import numpy as np
import ml_dtypes


def mxq(x, axis, fmt="e4m3"):
    dtype, down = {"e4m3": (ml_dtypes.float8_e4m3fn, 7), "e5m2": (ml_dtypes.float8_e5m2, 14)}[fmt]
    v = np.moveaxis(np.asarray(x, np.float32).astype(ml_dtypes.bfloat16).astype(np.float64), axis, -1)
    blocks = v.reshape(v.shape[:-1] + (-1, 32))
    amax = np.abs(blocks).max(-1, keepdims=True)
    byte = np.maximum(np.where(amax > 0, np.frexp(amax)[1] - 1 + 127, 0) - down, 1)
    scale = np.exp2(byte - 127.0)
    codes = (blocks / scale).astype(np.float32).astype(dtype).astype(np.float64)
    return np.moveaxis((codes * scale).reshape(v.shape), -1, axis)


WIDE = False


def mx_kscale(k):
    if not WIDE:
        return np.ones(k)
    levels = np.array([10, -10, 5, -5, 0])
    a = np.random.permutation(np.resize(levels, k // 512 * 4)).reshape(k // 512, 4)
    idx = np.arange(k)
    return np.exp2(a[idx // 512, idx % 128 // 32])


BF16 = ml_dtypes.bfloat16


def bf(x):
    return np.asarray(x, np.float32).astype(BF16)


def f64(x):
    return np.asarray(x).astype(np.float64)


B, S, E, H, HKV, D, F, M0, M1 = 1, 512, 1536, 32, 4, 128, 8192, 48, 40
REP = H // HKV


def setup_inputs():
    t = mx_kscale(H * D).reshape(HKV, REP, D)[:, :1, :]
    keep = (np.random.random_sample((B, 1, S, S)) < 0.7) | np.eye(S, dtype=bool)
    row = 0.5 + 1.5 * np.random.random_sample((B, S, 1))
    sgn = np.where(np.random.random_sample((B, HKV, 1, D)) < 0.5, -1.0, 1.0)
    return {"q_rot": bf(np.random.standard_normal((B, H, S, D))),
            "k_rot": bf(np.random.standard_normal((B, HKV, S, D))),
            "v": bf(np.abs(np.random.standard_normal((B, HKV, S, D))) * sgn * t),
            "attention_mask": bf(np.where(keep, 0.5 * np.random.standard_normal((B, 1, S, S)), -1e9)),
            "wo": bf(np.random.standard_normal((E, H * D)) * 4.0 / np.sqrt(H * D) / np.broadcast_to(t, (HKV, REP, D)).reshape(H * D)),
            "x": bf(np.random.standard_normal((B, S, E)) * row)}


def reference(q_rot, k_rot, v, attention_mask, wo, x):
    qg = f64(q_rot).reshape(B, HKV, REP * S, D)
    s = (qg @ f64(k_rot).transpose(0, 1, 3, 2)).reshape(B, H, S, S) / np.sqrt(D) + f64(attention_mask)
    e = np.exp(s - s.max(-1, keepdims=True))
    o = (mxq(e.reshape(B, HKV, REP * S, S), 3, "e4m3") @ mxq(f64(v), 2, "e4m3")).reshape(B, H, S, D) / e.sum(-1, keepdims=True)
    attn = o.transpose(0, 2, 1, 3).reshape(B, S, H * D)
    return f64(x) + (mxq(attn, 2, "e4m3") @ mxq(f64(wo), 1, "e4m3").T)

@@ -1,0 +1,323 @@
+from contextlib import ExitStack
+import math
+
+import concourse.mybir as mybir
+from concourse.masks import make_identity
+
+F32 = mybir.dt.float32
+BF16 = mybir.dt.bfloat16
+U32 = mybir.dt.uint32
+U8 = mybir.dt.uint8
+FP8X4 = mybir.dt.float8_e4m3fn_x4
+ALU = mybir.AluOpType
+ACTF = mybir.ActivationFunctionType
+AXIS = mybir.AxisListType
+
+P = 128
+H = 32
+HKV = 4
+S = 512
+D = 128
+E = 1536
+C = H * D
+NQB = S // P
+UNITS_PER_QB = 8
+NUNITS = NQB * UNITS_PER_QB
+FLOPS = 2 * H * S * S * D * 2 + 2 * S * C * E
+
+PE_ADD_MOD = 4
+GP_E = True
+GP_A = True
+NORM_ON_V = True
+S_BUFS = 3
+MISC_BUFS = 1
+PIN = False
+
+
+def tile_selectivetransformerlayer_pb_kernel(tc, q_rot, k_rot, v, attention_mask, wo, x, out):
+    nc = tc.nc
+    scale = 1.0 / math.sqrt(D)
+    q_v = q_rot.rearrange("b h (n p) d -> p n (b h) d", p=P)
+    k_v = k_rot.rearrange("b g (n p) d -> p (b g n) d", p=P)
+    v_v = v.rearrange("b g (t p) d -> p (b g t) d", p=P)
+    m_v = attention_mask.rearrange("a b (n p) k -> p (a b n) k", p=P)
+    wo_v = wo.rearrange("(n p) c -> p n c", p=P)
+    x_v = x.rearrange("b (n p) e -> p (b n) e", p=P)
+    out_v = out.rearrange("b (n p) e -> p (b n) e", p=P)
+
+    with ExitStack() as ctx:
+        keep = ctx.enter_context(tc.tile_pool(name="keep", bufs=1))
+        work = ctx.enter_context(tc.tile_pool(name="work", bufs=2))
+        small = ctx.enter_context(tc.tile_pool(name="small", bufs=4))
+        psum = ctx.enter_context(tc.psum_pool(name="psum", bufs=1))
+        if PIN:
+            ctx.enter_context(tc.manual_schedule())
+
+        k_raw = keep.tile([P, HKV * 4, D], BF16)
+        nc.sync.dma_start(out=k_raw[:], in_=k_v)
+        q_raws = {}
+
+        def load_q(qb):
+            q_raw = work.tile([P, H, D], BF16, tag="q_raw")
+            for c4 in range(4):
+                nc.sync.dma_start(out=q_raw[:, c4 * 8:(c4 + 1) * 8, :], in_=q_v[:, qb, c4 * 8:(c4 + 1) * 8, :])
+            q_raws[qb] = q_raw
+
+        load_q(0)
+        mask_sb = keep.tile([P, NQB, S], BF16)
+        nc.sync.dma_start(out=mask_sb[:], in_=m_v)
+        v_raw = keep.tile([P, HKV, 4, D], BF16)
+        nc.sync.dma_start(out=v_raw[:].rearrange("p g t d -> p (g t) d"), in_=v_v)
+
+        ident_bf = keep.tile([P, P], BF16)
+        make_identity(nc, ident_bf[:])
+        ident_f = keep.tile([P, P], F32)
+        make_identity(nc, ident_f[:])
+
+        kT = keep.tile([P, HKV * S], BF16)
+        for half in range(2):
+            ps_k = psum.tile([P, 8 * P], BF16, tag="misc", bufs=MISC_BUFS)
+            for i in range(8):
+                nc.tensor.transpose(ps_k[:, i * P:(i + 1) * P], k_raw[:, half * 8 + i, :], ident_bf[:])
+            nc.vector.tensor_copy(out=kT[:, half * 1024:(half + 1) * 1024], in_=ps_k[:])
+
+        maskT = None
+        if PE_ADD_MOD > 0:
+            maskT = keep.tile([P, NQB, 4, P], F32)
+            for half in range(2):
+                ps_m = psum.tile([P, 8 * P], BF16, tag="misc", bufs=MISC_BUFS)
+                for i in range(8):
+                    qb, kb = divmod(half * 8 + i, 4)
+                    nc.tensor.transpose(ps_m[:, i * P:(i + 1) * P], mask_sb[:, qb, kb * P:(kb + 1) * P], ident_bf[:])
+                nc.vector.tensor_scalar_mul(
+                    out=maskT[:, half * 2:(half + 1) * 2, :, :].rearrange("p a b q -> p (a b q)"),
+                    in0=ps_m[:], scalar1=math.sqrt(D))
+
+        v_grp = keep.tile([P, HKV, D, 4], BF16, align_bytes=64)
+        nc.vector.tensor_copy(out=v_grp[:], in_=v_raw[:].rearrange("p g t d -> p g d t"))
+        vcodes = keep.tile([P, HKV * D], U32, align_bytes=64)
+        vscales = keep.tile([P, HKV * D], U8, align_bytes=64)
+        nc.vector.quantize_mx(out=vcodes[:].bitcast(FP8X4), scales=vscales[:],
+                              in_=v_grp[:].rearrange("p g d t -> p (g d t)"))
+
+        wcodes = keep.tile([P, 8, E], U32, align_bytes=64)
+        wscales = keep.tile([P, 8, E], U8, align_bytes=64)
+        wo_raws = {}
+
+        def load_wo(pr):
+            for i in range(2):
+                wo_raw = work.tile([P, C], BF16, tag="wo_raw", bufs=4)
+                nc.sync.dma_start(out=wo_raw[:], in_=wo_v[:, pr * 2 + i, :])
+                wo_raws[pr * 2 + i] = wo_raw
+
+        def wstep(pr, g):
+            ps_w = psum.tile([P, 2, 2 * P], F32, tag="misc", bufs=MISC_BUFS)
+            for i in range(2):
+                w32 = wo_raws[pr * 2 + i][:].bitcast(F32)
+                for u in range(2):
+                    lo = g * 256 + u * P
+                    nc.tensor.transpose(ps_w[:, u, i * P:(i + 1) * P], w32[:, lo:lo + P], ident_f[:])
+            wg = work.tile([P, 1024], BF16, tag="wg", align_bytes=64)
+            nc.scalar.copy(out=wg[:].bitcast(F32).rearrange("p (e u) -> p e u", u=2),
+                           in_=ps_w[:].rearrange("p u e -> p e u"))
+            nc.vector.quantize_mx(out=wcodes[:, g, pr * 256:(pr + 1) * 256].bitcast(FP8X4),
+                                  scales=wscales[:, g, pr * 256:(pr + 1) * 256], in_=wg[:])
+
+        load_wo(0)
+        load_wo(1)
+
+        st = {}
+        qbst = {0: {}, 1: {}, 2: {}, 3: {}}
+
+        def stage_q(n):
+            qb, a = divmod(n, UNITS_PER_QB)
+            ps_q = psum.tile([P, 4, P], BF16, tag="misc", bufs=MISC_BUFS)
+            for j in range(4):
+                nc.tensor.transpose(ps_q[:, j, :], q_raws[qb][:, 4 * a + j, :], ident_bf[:])
+            qT = work.tile([P, 4, P], BF16, tag="qT", bufs=3)
+            nc.scalar.copy(out=qT[:], in_=ps_q[:])
+            st[n] = {"qT": qT}
+
+        def stage_s(n):
+            qb, a = divmod(n, UNITS_PER_QB)
+            g = a // 2
+            qT = st[n]["qT"]
+            e = work.tile([P, 4, S], BF16, tag="e", bufs=3)
+            rowsum = small.tile([P, 4], F32, tag="rowsum")
+            nv = 4 - PE_ADD_MOD
+            srcs = {}
+            negm = None
+            if PE_ADD_MOD > 0:
+                negm = small.tile([P, PE_ADD_MOD], F32, tag="negm")
+            for j in range(PE_ADD_MOD):
+                ps_s = psum.tile([P, S], F32, tag="s", bufs=S_BUFS)
+                nc.tensor.matmul(out=ps_s[:], lhsT=qT[:, j, :], rhs=kT[:, g * S:(g + 1) * S], start=True, stop=False)
+                for kb in range(4):
+                    nc.tensor.matmul(out=ps_s[:, kb * P:(kb + 1) * P], lhsT=maskT[:, qb, kb, :], rhs=ident_f[:],
+                                     is_transpose=True, start=False, stop=(kb == 3))
+                junk = work.tile([P, S], BF16, tag="junk")
+                nc.vector.tensor_scalar(out=junk[:], in0=ps_s[:], scalar1=-scale, scalar2=None,
+                                        op0=ALU.mult, op1=ALU.min, accum_out=negm[:, j:j + 1])
+                srcs[j] = ps_s
+            if nv > 0:
+                t = work.tile([P, nv, S], F32, tag="t")
+                for j in range(PE_ADD_MOD, 4):
+                    ps_s = psum.tile([P, S], F32, tag="s", bufs=S_BUFS)
+                    nc.tensor.matmul(out=ps_s[:], lhsT=qT[:, j, :], rhs=kT[:, g * S:(g + 1) * S], start=True, stop=True)
+                    nc.vector.scalar_tensor_tensor(out=t[:, j - PE_ADD_MOD, :], in0=ps_s[:], scalar=scale,
+                                                   in1=mask_sb[:, qb, :], op0=ALU.mult, op1=ALU.add)
+                mx = small.tile([P, nv], F32, tag="mx")
+                nc.vector.tensor_reduce(out=mx[:], in_=t[:], axis=AXIS.X, op=ALU.max)
+                negv = small.tile([P, nv], F32, tag="negv")
+                nc.vector.tensor_scalar_mul(out=negv[:], in0=mx[:], scalar1=-1.0)
+            for j in range(4):
+                if j < PE_ADD_MOD:
+                    nc.scalar.activation(out=e[:, j, :], in_=srcs[j][:], func=ACTF.Exp, bias=negm[:, j:j + 1],
+                                         scale=scale, accum_out=rowsum[:, j:j + 1])
+                else:
+                    jv = j - PE_ADD_MOD
+                    nc.scalar.activation(out=e[:, j, :], in_=t[:, jv, :], func=ACTF.Exp, bias=negv[:, jv:jv + 1],
+                                         scale=1.0, accum_out=rowsum[:, j:j + 1])
+            st[n]["e"] = e
+            st[n]["rowsum"] = rowsum
+
+        def stage_t(n):
+            e = st[n]["e"]
+            grp = work.tile([P, 4, P, 4], BF16, tag="grp", align_bytes=64)
+            stage = None
+            if GP_E:
+                stage = work.tile([P, 4, 4, P], BF16, tag="stage")
+            for jj in range(2):
+                ps_t = psum.tile([P, 2, 4, P], BF16, tag="tr", bufs=2)
+                for i in range(2):
+                    for t4 in range(4):
+                        nc.tensor.transpose(ps_t[:, i, t4, :], e[:, 2 * jj + i, t4 * P:(t4 + 1) * P], ident_bf[:])
+                if GP_E:
+                    nc.scalar.copy(out=stage[:, 2 * jj:2 * jj + 2, :, :], in_=ps_t[:])
+                else:
+                    nc.scalar.copy(out=grp[:, 2 * jj:2 * jj + 2, :, :], in_=ps_t[:].rearrange("p i t q -> p i q t"))
+            if GP_E:
+                nc.gpsimd.tensor_scalar(out=grp[:], in0=stage[:].rearrange("p j t q -> p j q t"),
+                                        scalar1=1.0, scalar2=0.0, op0=ALU.mult, op1=ALU.add)
+            ecodes = work.tile([P, 4 * P], U32, tag="ecodes", align_bytes=64)
+            escales = work.tile([P, 4 * P], U8, tag="escales", align_bytes=64)
+            nc.vector.quantize_mx(out=ecodes[:].bitcast(FP8X4), scales=escales[:],
+                                  in_=grp[:].rearrange("p j q t -> p (j q t)"))
+            st[n]["ecodes"] = ecodes
+            st[n]["escales"] = escales
+
+        def stage_o(n):
+            qb, a = divmod(n, UNITS_PER_QB)
+            g = a // 2
+            gi = a % 2
+            ecodes = st[n]["ecodes"]
+            escales = st[n]["escales"]
+            ps_o = psum.tile([P, 4, P], F32, tag="o")
+            for j in range(4):
+                nc.tensor.matmul_mx(out=ps_o[:, j, :],
+                                    lhsT=ecodes[:, j * P:(j + 1) * P].bitcast(FP8X4),
+                                    lhsT_scale=escales[:, j * P:(j + 1) * P],
+                                    rhs=vcodes[:, g * D:(g + 1) * D].bitcast(FP8X4),
+                                    rhs_scale=vscales[:, g * D:(g + 1) * D],
+                                    start=True, stop=True)
+            r = small.tile([P, 4], F32, tag="r")
+            nc.vector.reciprocal(out=r[:], in_=st[n]["rowsum"][:])
+            if a == 0:
+                acodes = work.tile([P, 8 * P], U32, tag="acodes", align_bytes=64)
+                ascales = work.tile([P, 8 * P], U8, tag="ascales", align_bytes=64)
+                qbst[qb]["acodes"] = acodes
+                qbst[qb]["ascales"] = ascales
+            if gi == 0:
+                attn2 = work.tile([P, 2, 4, P], BF16, tag="attn2")
+                qbst[qb]["attn2"] = attn2
+            attn2 = qbst[qb]["attn2"]
+            if NORM_ON_V:
+                for ee in range(2):
+                    nc.vector.tensor_tensor(
+                        out=attn2[:, gi, :, :].rearrange("p (u e) (hh pp) -> p e u hh pp", e=2, hh=2)[:, ee],
+                        in0=ps_o[:].rearrange("p (u hh) (pp e) -> p e u hh pp", hh=2, e=2)[:, ee],
+                        in1=r[:].rearrange("p (u hh) -> p u hh", hh=2).unsqueeze(3).to_broadcast([P, 2, 2, 64]),
+                        op=ALU.mult)
+            else:
+                for j in range(4):
+                    u, hh = divmod(j, 2)
+                    nc.scalar.activation(out=attn2[:, gi, 2 * u:2 * u + 2, hh * 64:(hh + 1) * 64],
+                                         in_=ps_o[:, j, :].rearrange("p (pp e) -> p e pp", e=2),
+                                         func=ACTF.Copy, scale=r[:, j:j + 1])
+            if gi == 1:
+                ps_a = psum.tile([P, 2, 4, P], BF16, tag="tr", bufs=2)
+                for i in range(2):
+                    for t4 in range(4):
+                        nc.tensor.transpose(ps_a[:, i, t4, :], attn2[:, i, t4, :], ident_bf[:])
+                ag = work.tile([P, 2, P, 4], BF16, tag="ag", align_bytes=64)
+                if GP_A:
+                    astage = work.tile([P, 2, 4, P], BF16, tag="astage")
+                    nc.scalar.copy(out=astage[:], in_=ps_a[:])
+                    nc.gpsimd.tensor_scalar(out=ag[:], in0=astage[:].rearrange("p i t q -> p i q t"),
+                                            scalar1=1.0, scalar2=0.0, op0=ALU.mult, op1=ALU.add)
+                else:
+                    nc.scalar.copy(out=ag[:], in_=ps_a[:].rearrange("p i t q -> p i q t"))
+                lo = (a - 1) * P
+                nc.vector.quantize_mx(out=qbst[qb]["acodes"][:, lo:lo + 2 * P].bitcast(FP8X4),
+                                      scales=qbst[qb]["ascales"][:, lo:lo + 2 * P],
+                                      in_=ag[:].rearrange("p i q t -> p (i q t)"))
+
+        def load_x(qb):
+            x_sb = work.tile([P, E], BF16, tag="x_sb")
+            nc.sync.dma_start(out=x_sb[:], in_=x_v[:, qb, :])
+            qbst[qb]["x"] = x_sb
+
+        def op_passes(qb, ps, ec, g_lo, g_hi):
+            for g in range(g_lo, g_hi):
+                nc.tensor.matmul_mx(out=ps[:],
+                                    lhsT=qbst[qb]["acodes"][:, g * P:(g + 1) * P].bitcast(FP8X4),
+                                    lhsT_scale=qbst[qb]["ascales"][:, g * P:(g + 1) * P],
+                                    rhs=wcodes[:, g, ec * 512:(ec + 1) * 512].bitcast(FP8X4),
+                                    rhs_scale=wscales[:, g, ec * 512:(ec + 1) * 512],
+                                    start=(g == 0), stop=(g == 7))
+
+        def op_finish(qb, ps, ec):
+            o_sb = work.tile([P, 512], F32, tag="o_sb", bufs=3)
+            nc.vector.tensor_tensor(out=o_sb[:], in0=ps[:], in1=qbst[qb]["x"][:, ec * 512:(ec + 1) * 512], op=ALU.add)
+            nc.sync.dma_start(out=out_v[:, qb, ec * 512:(ec + 1) * 512], in_=o_sb[:])
+
+        def outproj(qb):
+            for ec in range(3):
+                ps_p = psum.tile([P, 512], F32, tag="op")
+                op_passes(qb, ps_p, ec, 0, 8)
+                op_finish(qb, ps_p, ec)
+
+        wlist = [(pr, g) for pr in range(6) for g in range(8)]
+        wpos = 0
+        stage_q(0)
+        for n in range(NUNITS + 2):
+            if n - 2 >= 0:
+                stage_o(n - 2)
+            if n - 1 >= 0 and n - 1 < NUNITS:
+                stage_t(n - 1)
+            if n < NUNITS:
+                stage_s(n)
+            if n + 1 < NUNITS:
+                stage_q(n + 1)
+            if n % UNITS_PER_QB == 1 and n // UNITS_PER_QB + 1 < NQB:
+                load_q(n // UNITS_PER_QB + 1)
+            for rep in range(3):
+                if wpos < len(wlist):
+                    pr, g = wlist[wpos]
+                    wstep(pr, g)
+                    wpos += 1
+                    if g == 7 and pr + 2 < 6:
+                        load_wo(pr + 2)
+            if n == 10:
+                load_x(0)
+            if n == 14:
+                load_x(1)
+            if n == 17:
+                outproj(0)
+                load_x(2)
+            if n == 21:
+                outproj(1)
+                load_x(3)
+            if n == 27:
+                outproj(2)
+        outproj(3)

@@ -25,12 +25,12 @@ UNITS_PER_QB = 8
 NUNITS = NQB * UNITS_PER_QB
 FLOPS = 2 * H * S * S * D * 2 + 2 * S * C * E
 
-PE_ADD_MOD = 4
-GP_E = True
-GP_A = True
+PE_ADD_MOD = 0
+GP_E = False
+GP_A = False
 NORM_ON_V = True
-S_BUFS = 3
-MISC_BUFS = 1
+S_BUFS = 2
+MISC_BUFS = 2
 PIN = False
 
 

@@ -25,13 +25,15 @@ UNITS_PER_QB = 8
 NUNITS = NQB * UNITS_PER_QB
 FLOPS = 2 * H * S * S * D * 2 + 2 * S * C * E
 
-PE_ADD_MOD = 0
-GP_E = False
-GP_A = False
-NORM_ON_V = True
-S_BUFS = 2
-MISC_BUFS = 2
-PIN = False
+GP_E = True
+GP_A = True
+NORM_ON_V = False
+PIN = True
+HIDE = 3
+W_PLAN = (1, 2, 1, 1)
+NPAIR = 64
+W_START = 4
+GP_TAIL = 4
 
 
 def tile_selectivetransformerlayer_pb_kernel(tc, q_rot, k_rot, v, attention_mask, wo, x, out):
@@ -47,27 +49,37 @@ def tile_selectivetransformerlayer_pb_kernel(tc, q_rot, k_rot, v, attention_mask
 
     with ExitStack() as ctx:
         keep = ctx.enter_context(tc.tile_pool(name="keep", bufs=1))
-        work = ctx.enter_context(tc.tile_pool(name="work", bufs=2))
-        small = ctx.enter_context(tc.tile_pool(name="small", bufs=4))
+        work = ctx.enter_context(tc.tile_pool(name="work", bufs=3))
+        small = ctx.enter_context(tc.tile_pool(name="small", bufs=12))
         psum = ctx.enter_context(tc.psum_pool(name="psum", bufs=1))
         if PIN:
             ctx.enter_context(tc.manual_schedule())
 
         k_raw = keep.tile([P, HKV * 4, D], BF16)
-        nc.sync.dma_start(out=k_raw[:], in_=k_v)
+        mask_sb = keep.tile([P, NQB, S], BF16)
+        v_raw = keep.tile([P, HKV, 4, D], BF16)
         q_raws = {}
 
+        def load_q_part(qb, c4):
+            nc.sync.dma_start(out=q_raws[qb][:, c4 * 8:(c4 + 1) * 8, :], in_=q_v[:, qb, c4 * 8:(c4 + 1) * 8, :])
+
         def load_q(qb):
-            q_raw = work.tile([P, H, D], BF16, tag="q_raw")
-            for c4 in range(4):
-                nc.sync.dma_start(out=q_raw[:, c4 * 8:(c4 + 1) * 8, :], in_=q_v[:, qb, c4 * 8:(c4 + 1) * 8, :])
+            q_raw = work.tile([P, H, D], BF16, tag="q_raw", bufs=2)
             q_raws[qb] = q_raw
+            if qb > 0:
+                for c4 in range(4):
+                    load_q_part(qb, c4)
 
         load_q(0)
-        mask_sb = keep.tile([P, NQB, S], BF16)
-        nc.sync.dma_start(out=mask_sb[:], in_=m_v)
-        v_raw = keep.tile([P, HKV, 4, D], BF16)
+        nc.sync.dma_start(out=k_raw[:, 0:4, :], in_=k_v[:, 0:4, :])
+        load_q_part(0, 0)
+        nc.sync.dma_start(out=mask_sb[:, 0:1, :], in_=m_v[:, 0:1, :])
+        nc.sync.dma_start(out=k_raw[:, 4:16, :], in_=k_v[:, 4:16, :])
+        load_q_part(0, 1)
         nc.sync.dma_start(out=v_raw[:].rearrange("p g t d -> p (g t) d"), in_=v_v)
+        load_q_part(0, 2)
+        load_q_part(0, 3)
+        nc.sync.dma_start(out=mask_sb[:, 1:4, :], in_=m_v[:, 1:4, :])
 
         ident_bf = keep.tile([P, P], BF16)
         make_identity(nc, ident_bf[:])
@@ -75,33 +87,30 @@ def tile_selectivetransformerlayer_pb_kernel(tc, q_rot, k_rot, v, attention_mask
         make_identity(nc, ident_f[:])
 
         kT = keep.tile([P, HKV * S], BF16)
-        for half in range(2):
-            ps_k = psum.tile([P, 8 * P], BF16, tag="misc", bufs=MISC_BUFS)
-            for i in range(8):
-                nc.tensor.transpose(ps_k[:, i * P:(i + 1) * P], k_raw[:, half * 8 + i, :], ident_bf[:])
-            nc.vector.tensor_copy(out=kT[:, half * 1024:(half + 1) * 1024], in_=ps_k[:])
+        KS = {}
 
-        maskT = None
-        if PE_ADD_MOD > 0:
-            maskT = keep.tile([P, NQB, 4, P], F32)
-            for half in range(2):
-                ps_m = psum.tile([P, 8 * P], BF16, tag="misc", bufs=MISC_BUFS)
-                for i in range(8):
-                    qb, kb = divmod(half * 8 + i, 4)
-                    nc.tensor.transpose(ps_m[:, i * P:(i + 1) * P], mask_sb[:, qb, kb * P:(kb + 1) * P], ident_bf[:])
-                nc.vector.tensor_scalar_mul(
-                    out=maskT[:, half * 2:(half + 1) * 2, :, :].rearrange("p a b q -> p (a b q)"),
-                    in0=ps_m[:], scalar1=math.sqrt(D))
+        def pe_kt_list(g):
+            ps_k = psum.tile([P, 4, P], BF16, tag="misc", bufs=2)
+            KS[g] = ps_k
+            return [(ps_k[:, i, :], k_raw[:, g * 4 + i, :]) for i in range(4)]
+
+        def s_kcopy(g):
+            nc.scalar.copy(out=kT[:, g * S:(g + 1) * S], in_=KS[g][:].rearrange("p i k -> p (i k)"))
 
         v_grp = keep.tile([P, HKV, D, 4], BF16, align_bytes=64)
-        nc.vector.tensor_copy(out=v_grp[:], in_=v_raw[:].rearrange("p g t d -> p g d t"))
         vcodes = keep.tile([P, HKV * D], U32, align_bytes=64)
         vscales = keep.tile([P, HKV * D], U8, align_bytes=64)
-        nc.vector.quantize_mx(out=vcodes[:].bitcast(FP8X4), scales=vscales[:],
-                              in_=v_grp[:].rearrange("p g d t -> p (g d t)"))
+
+        def v_prep_copy():
+            nc.vector.tensor_copy(out=v_grp[:], in_=v_raw[:].rearrange("p g t d -> p g d t"))
+
+        def v_prep_quant():
+            nc.vector.quantize_mx(out=vcodes[:].bitcast(FP8X4), scales=vscales[:],
+                                  in_=v_grp[:].rearrange("p g d t -> p (g d t)"))
 
         wcodes = keep.tile([P, 8, E], U32, align_bytes=64)
         wscales = keep.tile([P, 8, E], U8, align_bytes=64)
+        x_sb = keep.tile([P, NQB, E], BF16)
         wo_raws = {}
 
         def load_wo(pr):
@@ -110,214 +119,310 @@ def tile_selectivetransformerlayer_pb_kernel(tc, q_rot, k_rot, v, attention_mask
                 nc.sync.dma_start(out=wo_raw[:], in_=wo_v[:, pr * 2 + i, :])
                 wo_raws[pr * 2 + i] = wo_raw
 
-        def wstep(pr, g):
-            ps_w = psum.tile([P, 2, 2 * P], F32, tag="misc", bufs=MISC_BUFS)
-            for i in range(2):
-                w32 = wo_raws[pr * 2 + i][:].bitcast(F32)
-                for u in range(2):
-                    lo = g * 256 + u * P
-                    nc.tensor.transpose(ps_w[:, u, i * P:(i + 1) * P], w32[:, lo:lo + P], ident_f[:])
-            wg = work.tile([P, 1024], BF16, tag="wg", align_bytes=64)
-            nc.scalar.copy(out=wg[:].bitcast(F32).rearrange("p (e u) -> p e u", u=2),
-                           in_=ps_w[:].rearrange("p u e -> p e u"))
-            nc.vector.quantize_mx(out=wcodes[:, g, pr * 256:(pr + 1) * 256].bitcast(FP8X4),
-                                  scales=wscales[:, g, pr * 256:(pr + 1) * 256], in_=wg[:])
-
         load_wo(0)
         load_wo(1)
 
-        st = {}
-        qbst = {0: {}, 1: {}, 2: {}, 3: {}}
+        PS = {}
+        US = {}
+        RS = {}
+        QS = {0: {}, 1: {}, 2: {}, 3: {}}
+        WS = {}
 
-        def stage_q(n):
-            qb, a = divmod(n, UNITS_PER_QB)
-            ps_q = psum.tile([P, 4, P], BF16, tag="misc", bufs=MISC_BUFS)
-            for j in range(4):
-                nc.tensor.transpose(ps_q[:, j, :], q_raws[qb][:, 4 * a + j, :], ident_bf[:])
-            qT = work.tile([P, 4, P], BF16, tag="qT", bufs=3)
-            nc.scalar.copy(out=qT[:], in_=ps_q[:])
-            st[n] = {"qT": qT}
+        def tr_bf(pair):
+            nc.tensor.transpose(pair[0], pair[1], ident_bf[:])
 
-        def stage_s(n):
-            qb, a = divmod(n, UNITS_PER_QB)
-            g = a // 2
-            qT = st[n]["qT"]
-            e = work.tile([P, 4, S], BF16, tag="e", bufs=3)
-            rowsum = small.tile([P, 4], F32, tag="rowsum")
-            nv = 4 - PE_ADD_MOD
-            srcs = {}
-            negm = None
-            if PE_ADD_MOD > 0:
-                negm = small.tile([P, PE_ADD_MOD], F32, tag="negm")
-            for j in range(PE_ADD_MOD):
-                ps_s = psum.tile([P, S], F32, tag="s", bufs=S_BUFS)
-                nc.tensor.matmul(out=ps_s[:], lhsT=qT[:, j, :], rhs=kT[:, g * S:(g + 1) * S], start=True, stop=False)
-                for kb in range(4):
-                    nc.tensor.matmul(out=ps_s[:, kb * P:(kb + 1) * P], lhsT=maskT[:, qb, kb, :], rhs=ident_f[:],
-                                     is_transpose=True, start=False, stop=(kb == 3))
-                junk = work.tile([P, S], BF16, tag="junk")
-                nc.vector.tensor_scalar(out=junk[:], in0=ps_s[:], scalar1=-scale, scalar2=None,
-                                        op0=ALU.mult, op1=ALU.min, accum_out=negm[:, j:j + 1])
-                srcs[j] = ps_s
-            if nv > 0:
-                t = work.tile([P, nv, S], F32, tag="t")
-                for j in range(PE_ADD_MOD, 4):
-                    ps_s = psum.tile([P, S], F32, tag="s", bufs=S_BUFS)
-                    nc.tensor.matmul(out=ps_s[:], lhsT=qT[:, j, :], rhs=kT[:, g * S:(g + 1) * S], start=True, stop=True)
-                    nc.vector.scalar_tensor_tensor(out=t[:, j - PE_ADD_MOD, :], in0=ps_s[:], scalar=scale,
-                                                   in1=mask_sb[:, qb, :], op0=ALU.mult, op1=ALU.add)
-                mx = small.tile([P, nv], F32, tag="mx")
-                nc.vector.tensor_reduce(out=mx[:], in_=t[:], axis=AXIS.X, op=ALU.max)
-                negv = small.tile([P, nv], F32, tag="negv")
-                nc.vector.tensor_scalar_mul(out=negv[:], in0=mx[:], scalar1=-1.0)
-            for j in range(4):
-                if j < PE_ADD_MOD:
-                    nc.scalar.activation(out=e[:, j, :], in_=srcs[j][:], func=ACTF.Exp, bias=negm[:, j:j + 1],
-                                         scale=scale, accum_out=rowsum[:, j:j + 1])
-                else:
-                    jv = j - PE_ADD_MOD
-                    nc.scalar.activation(out=e[:, j, :], in_=t[:, jv, :], func=ACTF.Exp, bias=negv[:, jv:jv + 1],
-                                         scale=1.0, accum_out=rowsum[:, j:j + 1])
-            st[n]["e"] = e
-            st[n]["rowsum"] = rowsum
+        def pe_qt_list(u):
+            qb, a = divmod(u, UNITS_PER_QB)
+            ps_q = psum.tile([P, 4, P], BF16, tag="misc", bufs=2)
+            US[u] = {"ps_q": ps_q}
+            return [(ps_q[:, j, :], q_raws[qb][:, 4 * a + j, :]) for j in range(4)]
 
-        def stage_t(n):
-            e = st[n]["e"]
-            grp = work.tile([P, 4, P, 4], BF16, tag="grp", align_bytes=64)
-            stage = None
-            if GP_E:
-                stage = work.tile([P, 4, 4, P], BF16, tag="stage")
-            for jj in range(2):
-                ps_t = psum.tile([P, 2, 4, P], BF16, tag="tr", bufs=2)
-                for i in range(2):
-                    for t4 in range(4):
-                        nc.tensor.transpose(ps_t[:, i, t4, :], e[:, 2 * jj + i, t4 * P:(t4 + 1) * P], ident_bf[:])
-                if GP_E:
-                    nc.scalar.copy(out=stage[:, 2 * jj:2 * jj + 2, :, :], in_=ps_t[:])
-                else:
-                    nc.scalar.copy(out=grp[:, 2 * jj:2 * jj + 2, :, :], in_=ps_t[:].rearrange("p i t q -> p i q t"))
-            if GP_E:
-                nc.gpsimd.tensor_scalar(out=grp[:], in0=stage[:].rearrange("p j t q -> p j q t"),
-                                        scalar1=1.0, scalar2=0.0, op0=ALU.mult, op1=ALU.add)
-            ecodes = work.tile([P, 4 * P], U32, tag="ecodes", align_bytes=64)
-            escales = work.tile([P, 4 * P], U8, tag="escales", align_bytes=64)
+        def s_qcopy(u):
+            qT = work.tile([P, 4, P], BF16, tag="qT")
+            nc.scalar.copy(out=qT[:], in_=US[u]["ps_q"][:])
+            US[u]["qT"] = qT
+
+        def pe_score(p, i):
+            u = p // 2
+            g = (u % UNITS_PER_QB) // 2
+            ps_s = psum.tile([P, S], F32, tag="s", bufs=2)
+            nc.tensor.matmul(out=ps_s[:], lhsT=US[u]["qT"][:, 2 * (p % 2) + i, :], rhs=kT[:, g * S:(g + 1) * S],
+                             start=True, stop=True)
+            PS[p]["ps_s%d" % i] = ps_s
+
+        def v_front(p):
+            qb = p // 16
+            t = work.tile([P, 2, S], F32, tag="t")
+            for i in range(2):
+                nc.vector.scalar_tensor_tensor(out=t[:, i, :], in0=PS[p]["ps_s%d" % i][:], scalar=-scale,
+                                               in1=mask_sb[:, qb, :], op0=ALU.mult, op1=ALU.subtract)
+            negm = small.tile([P, 2], F32, tag="negm")
+            nc.vector.tensor_reduce(out=negm[:], in_=t[:], axis=AXIS.X, op=ALU.min)
+            PS[p]["t"] = t
+            PS[p]["negm"] = negm
+
+        def s_exp(p):
+            e = work.tile([P, 2, S], BF16, tag="e")
+            rowsum = small.tile([P, 2], F32, tag="rowsum")
+            for i in range(2):
+                nc.scalar.activation(out=e[:, i, :], in_=PS[p]["t"][:, i, :], func=ACTF.Exp,
+                                     bias=PS[p]["negm"][:, i:i + 1], scale=-1.0, accum_out=rowsum[:, i:i + 1])
+            PS[p]["e"] = e
+            PS[p]["rowsum"] = rowsum
+
+        def pe_et_list(p):
+            ps_t = psum.tile([P, 2, 4, P], BF16, tag="tr", bufs=2)
+            PS[p]["ps_t"] = ps_t
+            e = PS[p]["e"]
+            return [(ps_t[:, i, t4, :], e[:, i, t4 * P:(t4 + 1) * P]) for i in range(2) for t4 in range(4)]
+
+        def s_fcopy(p):
+            ps_t = PS[p]["ps_t"]
+            if GP_E and p < NPAIR - GP_TAIL:
+                stage = work.tile([P, 2, 4, P], BF16, tag="stage")
+                nc.scalar.copy(out=stage[:], in_=ps_t[:])
+                PS[p]["stage"] = stage
+            else:
+                grp = work.tile([P, 2, P, 4], BF16, tag="grp", align_bytes=64)
+                nc.scalar.copy(out=grp[:], in_=ps_t[:].rearrange("p i t q -> p i q t"))
+                PS[p]["grp"] = grp
+
+        def g_regroup(p):
+            grp = work.tile([P, 2, P, 4], BF16, tag="grp", align_bytes=64)
+            nc.gpsimd.tensor_scalar(out=grp[:], in0=PS[p]["stage"][:].rearrange("p i t q -> p i q t"),
+                                    scalar1=1.0, scalar2=0.0, op0=ALU.mult, op1=ALU.add)
+            PS[p]["grp"] = grp
+
+        def v_quant(p):
+            ecodes = work.tile([P, 2 * P], U32, tag="ecodes", bufs=4, align_bytes=64)
+            escales = work.tile([P, 2 * P], U8, tag="escales", bufs=4, align_bytes=64)
             nc.vector.quantize_mx(out=ecodes[:].bitcast(FP8X4), scales=escales[:],
-                                  in_=grp[:].rearrange("p j q t -> p (j q t)"))
-            st[n]["ecodes"] = ecodes
-            st[n]["escales"] = escales
+                                  in_=PS[p]["grp"][:].rearrange("p i q t -> p (i q t)"))
+            r = small.tile([P, 2], F32, tag="r")
+            nc.vector.reciprocal(out=r[:], in_=PS[p]["rowsum"][:])
+            PS[p]["ecodes"] = ecodes
+            PS[p]["escales"] = escales
+            PS[p]["r"] = r
 
-        def stage_o(n):
-            qb, a = divmod(n, UNITS_PER_QB)
-            g = a // 2
-            gi = a % 2
-            ecodes = st[n]["ecodes"]
-            escales = st[n]["escales"]
+        def pe_pv(u):
+            g = (u % UNITS_PER_QB) // 2
             ps_o = psum.tile([P, 4, P], F32, tag="o")
             for j in range(4):
+                p, i = 2 * u + j // 2, j % 2
                 nc.tensor.matmul_mx(out=ps_o[:, j, :],
-                                    lhsT=ecodes[:, j * P:(j + 1) * P].bitcast(FP8X4),
-                                    lhsT_scale=escales[:, j * P:(j + 1) * P],
+                                    lhsT=PS[p]["ecodes"][:, i * P:(i + 1) * P].bitcast(FP8X4),
+                                    lhsT_scale=PS[p]["escales"][:, i * P:(i + 1) * P],
                                     rhs=vcodes[:, g * D:(g + 1) * D].bitcast(FP8X4),
                                     rhs_scale=vscales[:, g * D:(g + 1) * D],
                                     start=True, stop=True)
-            r = small.tile([P, 4], F32, tag="r")
-            nc.vector.reciprocal(out=r[:], in_=st[n]["rowsum"][:])
-            if a == 0:
-                acodes = work.tile([P, 8 * P], U32, tag="acodes", align_bytes=64)
-                ascales = work.tile([P, 8 * P], U8, tag="ascales", align_bytes=64)
-                qbst[qb]["acodes"] = acodes
-                qbst[qb]["ascales"] = ascales
-            if gi == 0:
-                attn2 = work.tile([P, 2, 4, P], BF16, tag="attn2")
-                qbst[qb]["attn2"] = attn2
-            attn2 = qbst[qb]["attn2"]
-            if NORM_ON_V:
-                for ee in range(2):
-                    nc.vector.tensor_tensor(
-                        out=attn2[:, gi, :, :].rearrange("p (u e) (hh pp) -> p e u hh pp", e=2, hh=2)[:, ee],
-                        in0=ps_o[:].rearrange("p (u hh) (pp e) -> p e u hh pp", hh=2, e=2)[:, ee],
-                        in1=r[:].rearrange("p (u hh) -> p u hh", hh=2).unsqueeze(3).to_broadcast([P, 2, 2, 64]),
-                        op=ALU.mult)
-            else:
-                for j in range(4):
-                    u, hh = divmod(j, 2)
-                    nc.scalar.activation(out=attn2[:, gi, 2 * u:2 * u + 2, hh * 64:(hh + 1) * 64],
-                                         in_=ps_o[:, j, :].rearrange("p (pp e) -> p e pp", e=2),
-                                         func=ACTF.Copy, scale=r[:, j:j + 1])
-            if gi == 1:
-                ps_a = psum.tile([P, 2, 4, P], BF16, tag="tr", bufs=2)
-                for i in range(2):
-                    for t4 in range(4):
-                        nc.tensor.transpose(ps_a[:, i, t4, :], attn2[:, i, t4, :], ident_bf[:])
-                ag = work.tile([P, 2, P, 4], BF16, tag="ag", align_bytes=64)
-                if GP_A:
-                    astage = work.tile([P, 2, 4, P], BF16, tag="astage")
-                    nc.scalar.copy(out=astage[:], in_=ps_a[:])
-                    nc.gpsimd.tensor_scalar(out=ag[:], in0=astage[:].rearrange("p i t q -> p i q t"),
-                                            scalar1=1.0, scalar2=0.0, op0=ALU.mult, op1=ALU.add)
-                else:
-                    nc.scalar.copy(out=ag[:], in_=ps_a[:].rearrange("p i t q -> p i q t"))
-                lo = (a - 1) * P
-                nc.vector.quantize_mx(out=qbst[qb]["acodes"][:, lo:lo + 2 * P].bitcast(FP8X4),
-                                      scales=qbst[qb]["ascales"][:, lo:lo + 2 * P],
-                                      in_=ag[:].rearrange("p i q t -> p (i q t)"))
+            US[u]["ps_o"] = ps_o
 
-        def load_x(qb):
-            x_sb = work.tile([P, E], BF16, tag="x_sb")
-            nc.sync.dma_start(out=x_sb[:], in_=x_v[:, qb, :])
-            qbst[qb]["x"] = x_sb
+        def norm(u):
+            rr = u // 2
+            gi = u % 2
+            if gi == 0:
+                attn2 = work.tile([P, 2, 4, P], BF16, tag="attn2", bufs=2)
+                RS[rr] = {"attn2": attn2}
+            attn2 = RS[rr]["attn2"]
+            ps_o = US[u]["ps_o"]
+            for j in range(4):
+                uu, hh = divmod(j, 2)
+                r = PS[2 * u + j // 2]["r"]
+                if NORM_ON_V:
+                    nc.vector.tensor_scalar_mul(out=attn2[:, gi, 2 * uu:2 * uu + 2, hh * 64:(hh + 1) * 64],
+                                                in0=ps_o[:, j, :].rearrange("p (pp e) -> p e pp", e=2),
+                                                scalar1=r[:, j % 2:j % 2 + 1])
+                else:
+                    nc.scalar.activation(out=attn2[:, gi, 2 * uu:2 * uu + 2, hh * 64:(hh + 1) * 64],
+                                         in_=ps_o[:, j, :].rearrange("p (pp e) -> p e pp", e=2),
+                                         func=ACTF.Copy, scale=r[:, j % 2:j % 2 + 1])
+
+        def pe_at_list(rr):
+            ps_a = psum.tile([P, 2, 4, P], BF16, tag="misc", bufs=2)
+            RS[rr]["ps_a"] = ps_a
+            attn2 = RS[rr]["attn2"]
+            return [(ps_a[:, i, t4, :], attn2[:, i, t4, :]) for i in range(2) for t4 in range(4)]
+
+        def s_acopy(rr):
+            if GP_A and rr < 14:
+                astage = work.tile([P, 2, 4, P], BF16, tag="astage", bufs=2)
+                nc.scalar.copy(out=astage[:], in_=RS[rr]["ps_a"][:])
+                RS[rr]["astage"] = astage
+            else:
+                ag = work.tile([P, 2, P, 4], BF16, tag="ag", bufs=2, align_bytes=64)
+                nc.scalar.copy(out=ag[:], in_=RS[rr]["ps_a"][:].rearrange("p i t q -> p i q t"))
+                RS[rr]["ag"] = ag
+
+        def g_aregroup(rr):
+            ag = work.tile([P, 2, P, 4], BF16, tag="ag", bufs=2, align_bytes=64)
+            nc.gpsimd.tensor_scalar(out=ag[:], in0=RS[rr]["astage"][:].rearrange("p i t q -> p i q t"),
+                                    scalar1=1.0, scalar2=0.0, op0=ALU.mult, op1=ALU.add)
+            RS[rr]["ag"] = ag
+
+        def v_aquant(rr):
+            qb, k4 = divmod(rr, 4)
+            if k4 == 0:
+                acodes = work.tile([P, 8 * P], U32, tag="acodes", bufs=4, align_bytes=64)
+                ascales = work.tile([P, 8 * P], U8, tag="ascales", bufs=4, align_bytes=64)
+                QS[qb]["acodes"] = acodes
+                QS[qb]["ascales"] = ascales
+            lo = k4 * 2 * P
+            nc.vector.quantize_mx(out=QS[qb]["acodes"][:, lo:lo + 2 * P].bitcast(FP8X4),
+                                  scales=QS[qb]["ascales"][:, lo:lo + 2 * P],
+                                  in_=RS[rr]["ag"][:].rearrange("p i q t -> p (i q t)"))
+
+        def pe_w(w):
+            pr, g = divmod(w, 8)
+            ps_w = psum.tile([P, 2, 2 * P], F32, tag="misc", bufs=2)
+            for i in range(2):
+                w32 = wo_raws[pr * 2 + i][:].bitcast(F32)
+                for uu in range(2):
+                    lo = g * 256 + uu * P
+                    nc.tensor.transpose(ps_w[:, uu, i * P:(i + 1) * P], w32[:, lo:lo + P], ident_f[:])
+            WS[w] = {"ps_w": ps_w}
+            if g == 7 and pr + 2 < 6:
+                load_wo(pr + 2)
+
+        def s_wcopy(w):
+            wg = work.tile([P, 1024], BF16, tag="wg", align_bytes=64)
+            nc.scalar.copy(out=wg[:].bitcast(F32).rearrange("p (e u) -> p e u", u=2),
+                           in_=WS[w]["ps_w"][:].rearrange("p u e -> p e u"))
+            WS[w]["wg"] = wg
+
+        def v_wquant(w):
+            pr, g = divmod(w, 8)
+            nc.vector.quantize_mx(out=wcodes[:, g, pr * 256:(pr + 1) * 256].bitcast(FP8X4),
+                                  scales=wscales[:, g, pr * 256:(pr + 1) * 256], in_=WS[w]["wg"][:])
 
         def op_passes(qb, ps, ec, g_lo, g_hi):
             for g in range(g_lo, g_hi):
                 nc.tensor.matmul_mx(out=ps[:],
-                                    lhsT=qbst[qb]["acodes"][:, g * P:(g + 1) * P].bitcast(FP8X4),
-                                    lhsT_scale=qbst[qb]["ascales"][:, g * P:(g + 1) * P],
+                                    lhsT=QS[qb]["acodes"][:, g * P:(g + 1) * P].bitcast(FP8X4),
+                                    lhsT_scale=QS[qb]["ascales"][:, g * P:(g + 1) * P],
                                     rhs=wcodes[:, g, ec * 512:(ec + 1) * 512].bitcast(FP8X4),
                                     rhs_scale=wscales[:, g, ec * 512:(ec + 1) * 512],
                                     start=(g == 0), stop=(g == 7))
 
         def op_finish(qb, ps, ec):
-            o_sb = work.tile([P, 512], F32, tag="o_sb", bufs=3)
-            nc.vector.tensor_tensor(out=o_sb[:], in0=ps[:], in1=qbst[qb]["x"][:, ec * 512:(ec + 1) * 512], op=ALU.add)
+            o_sb = work.tile([P, 512], F32, tag="o_sb")
+            nc.vector.tensor_tensor(out=o_sb[:], in0=ps[:], in1=x_sb[:, qb, ec * 512:(ec + 1) * 512], op=ALU.add)
             nc.sync.dma_start(out=out_v[:, qb, ec * 512:(ec + 1) * 512], in_=o_sb[:])
 
-        def outproj(qb):
-            for ec in range(3):
+        OQ = 5 if GP_E else 4
+        O_PV = OQ + 1
+        O_AT = O_PV + 2
+        O_AQ = O_AT + (3 if GP_A else 2)
+        state = {"w": 0}
+        w_slot = {}
+        aq_slot = {}
+        groups = [(qb, ec) for qb in range(NQB - 1) for ec in range(3)]
+        lastb = {}
+        fin_list = []
+        new_fin = []
+        K_SLOT = {-2: 0, 1: 1, 5: 2, 9: 3}
+        last = NPAIR + O_AQ + 1
+        s = -2
+        while s < last or groups or fin_list or new_fin or "done" not in lastb:
+            if s == 2:
+                v_prep_copy()
+            if s == 3:
+                v_prep_quant()
+            if 0 <= s - OQ < NPAIR:
+                v_quant(s - OQ)
+            for w in range(48):
+                if w_slot.get(w) == s - 2:
+                    v_wquant(w)
+            if (s - O_AQ) % 4 == 3 and 0 <= s - O_AQ < NPAIR:
+                v_aquant((s - O_AQ) // 4)
+                aq_slot[(s - O_AQ) // 4] = s
+            if NORM_ON_V and (s - O_PV - 1) % 2 == 1 and 0 <= s - O_PV - 1 < NPAIR:
+                norm((s - O_PV - 1) // 2)
+            pend = []
+            done_tr = 0
+            n_misc = 0
+            if 0 <= s - 2 < NPAIR:
+                pend.extend(pe_et_list(s - 2))
+            if s in K_SLOT:
+                pend.extend(pe_kt_list(K_SLOT[s]))
+                n_misc += 1
+            if s % 2 == 0 and 0 <= (s + 2) // 2 < NUNITS:
+                pend.extend(pe_qt_list((s + 2) // 2))
+                n_misc += 1
+            if (s - O_AT) % 4 == 3 and 0 <= s - O_AT < NPAIR:
+                pend.extend(pe_at_list((s - O_AT) // 4))
+                n_misc += 1
+            if 0 <= s < NPAIR:
+                PS[s] = {}
+                for i in range(2):
+                    pe_score(s, i)
+                    for rep in range(HIDE):
+                        if done_tr < len(pend):
+                            tr_bf(pend[done_tr])
+                            done_tr += 1
+            for pair in pend[done_tr:]:
+                tr_bf(pair)
+            if s >= W_START:
+                for rep in range(min(W_PLAN[s % 4], 2 - n_misc)):
+                    if state["w"] < 48:
+                        pe_w(state["w"])
+                        w_slot[state["w"]] = s
+                        state["w"] += 1
+            if (s - O_PV) % 2 == 1 and 0 <= s - O_PV < NPAIR:
+                pe_pv((s - O_PV) // 2)
+            ready = [gr for gr in groups
+                     if w_slot.get(16 * gr[1] + 15, 999) + 2 < s and aq_slot.get(4 * gr[0] + 3, 999) < s]
+            if ready and not fin_list:
+                qb, ec = ready[0]
+                groups = [gr for gr in groups if gr != (qb, ec)]
                 ps_p = psum.tile([P, 512], F32, tag="op")
                 op_passes(qb, ps_p, ec, 0, 8)
-                op_finish(qb, ps_p, ec)
-
-        wlist = [(pr, g) for pr in range(6) for g in range(8)]
-        wpos = 0
-        stage_q(0)
-        for n in range(NUNITS + 2):
-            if n - 2 >= 0:
-                stage_o(n - 2)
-            if n - 1 >= 0 and n - 1 < NUNITS:
-                stage_t(n - 1)
-            if n < NUNITS:
-                stage_s(n)
-            if n + 1 < NUNITS:
-                stage_q(n + 1)
-            if n % UNITS_PER_QB == 1 and n // UNITS_PER_QB + 1 < NQB:
-                load_q(n // UNITS_PER_QB + 1)
-            for rep in range(3):
-                if wpos < len(wlist):
-                    pr, g = wlist[wpos]
-                    wstep(pr, g)
-                    wpos += 1
-                    if g == 7 and pr + 2 < 6:
-                        load_wo(pr + 2)
-            if n == 10:
-                load_x(0)
-            if n == 14:
-                load_x(1)
-            if n == 17:
-                outproj(0)
-                load_x(2)
-            if n == 21:
-                outproj(1)
-                load_x(3)
-            if n == 27:
-                outproj(2)
-        outproj(3)
+                new_fin.append((qb, ps_p, ec))
+            if "ps" not in lastb and not groups and not fin_list and not new_fin and s >= NPAIR:
+                ps_l0 = psum.tile([P, 512], F32, tag="op")
+                ps_l1 = psum.tile([P, 512], F32, tag="s", bufs=2)
+                ps_l2 = psum.tile([P, 512], F32, tag="s", bufs=2)
+                lastb["ps"] = [ps_l0, ps_l1, ps_l2]
+                lastb["g"] = 0
+            while "ps" in lastb and lastb["g"] < 8 and aq_slot.get(12 + lastb["g"] // 2, 999) < s:
+                for ec in range(3):
+                    op_passes(NQB - 1, lastb["ps"][ec], ec, lastb["g"], lastb["g"] + 2)
+                    if lastb["g"] == 6:
+                        op_finish(NQB - 1, lastb["ps"][ec], ec)
+                lastb["g"] += 2
+                if lastb["g"] == 8:
+                    lastb["done"] = True
+            if 0 <= s < NPAIR:
+                v_front(s)
+            todo = fin_list[:]
+            fin_list = new_fin
+            new_fin = []
+            for item in todo:
+                op_finish(item[0], item[1], item[2])
+            if s - 1 in K_SLOT:
+                s_kcopy(K_SLOT[s - 1])
+            if s % 2 == 1 and 0 <= (s + 1) // 2 < NUNITS:
+                s_qcopy((s + 1) // 2)
+            for w in range(48):
+                if w_slot.get(w) == s - 1:
+                    s_wcopy(w)
+            if (s - O_AT - 1) % 4 == 3 and 0 <= s - O_AT - 1 < NPAIR:
+                s_acopy((s - O_AT - 1) // 4)
+            if 0 <= s - 3 < NPAIR:
+                s_fcopy(s - 3)
+            if 0 <= s - 1 < NPAIR:
+                s_exp(s - 1)
+            if (not NORM_ON_V) and (s - O_PV - 1) % 2 == 1 and 0 <= s - O_PV - 1 < NPAIR:
+                norm((s - O_PV - 1) // 2)
+            if GP_E and 0 <= s - 4 < NPAIR - GP_TAIL:
+                g_regroup(s - 4)
+            if GP_A and (s - O_AT - 2) % 4 == 3 and 0 <= s - O_AT - 2 < NPAIR - 8:
+                g_aregroup((s - O_AT - 2) // 4)
+            if s == 0:
+                load_q(1)
+            if s == 6:
+                nc.sync.dma_start(out=x_sb[:], in_=x_v)
+            if s == 13:
+                load_q(2)
+            if s == 29:
+                load_q(3)
+            s += 1

@@ -33,6 +33,8 @@ HIDE = 3
 W_PLAN = (1, 2, 1, 1)
 NPAIR = 64
 W_START = 4
+GRP_BUFS = 1
+AQ_LAG = 4
 GP_TAIL = 4
 
 
@@ -183,12 +185,12 @@ def tile_selectivetransformerlayer_pb_kernel(tc, q_rot, k_rot, v, attention_mask
                 nc.scalar.copy(out=stage[:], in_=ps_t[:])
                 PS[p]["stage"] = stage
             else:
-                grp = work.tile([P, 2, P, 4], BF16, tag="grp", align_bytes=64)
+                grp = work.tile([P, 2, P, 4], BF16, tag="grp_s", bufs=2, align_bytes=64)
                 nc.scalar.copy(out=grp[:], in_=ps_t[:].rearrange("p i t q -> p i q t"))
                 PS[p]["grp"] = grp
 
         def g_regroup(p):
-            grp = work.tile([P, 2, P, 4], BF16, tag="grp", align_bytes=64)
+            grp = work.tile([P, 2, P, 4], BF16, tag="grp", bufs=GRP_BUFS, align_bytes=64)
             nc.gpsimd.tensor_scalar(out=grp[:], in0=PS[p]["stage"][:].rearrange("p i t q -> p i q t"),
                                     scalar1=1.0, scalar2=0.0, op0=ALU.mult, op1=ALU.add)
             PS[p]["grp"] = grp
@@ -249,7 +251,7 @@ def tile_selectivetransformerlayer_pb_kernel(tc, q_rot, k_rot, v, attention_mask
                 nc.scalar.copy(out=astage[:], in_=RS[rr]["ps_a"][:])
                 RS[rr]["astage"] = astage
             else:
-                ag = work.tile([P, 2, P, 4], BF16, tag="ag", bufs=2, align_bytes=64)
+                ag = work.tile([P, 2, P, 4], BF16, tag="ag_s", bufs=2, align_bytes=64)
                 nc.scalar.copy(out=ag[:], in_=RS[rr]["ps_a"][:].rearrange("p i t q -> p i q t"))
                 RS[rr]["ag"] = ag
 
@@ -284,7 +286,7 @@ def tile_selectivetransformerlayer_pb_kernel(tc, q_rot, k_rot, v, attention_mask
                 load_wo(pr + 2)
 
         def s_wcopy(w):
-            wg = work.tile([P, 1024], BF16, tag="wg", align_bytes=64)
+            wg = work.tile([P, 1024], BF16, tag="wg", bufs=2, align_bytes=64)
             nc.scalar.copy(out=wg[:].bitcast(F32).rearrange("p (e u) -> p e u", u=2),
                            in_=WS[w]["ps_w"][:].rearrange("p u e -> p e u"))
             WS[w]["wg"] = wg
@@ -311,7 +313,7 @@ def tile_selectivetransformerlayer_pb_kernel(tc, q_rot, k_rot, v, attention_mask
         OQ = 5 if GP_E else 4
         O_PV = OQ + 1
         O_AT = O_PV + 2
-        O_AQ = O_AT + (3 if GP_A else 2)
+        O_AQ = O_AT + (AQ_LAG if GP_A else 2)
         state = {"w": 0}
         w_slot = {}
         aq_slot = {}
@@ -327,14 +329,14 @@ def tile_selectivetransformerlayer_pb_kernel(tc, q_rot, k_rot, v, attention_mask
                 v_prep_copy()
             if s == 3:
                 v_prep_quant()
-            if 0 <= s - OQ < NPAIR:
-                v_quant(s - OQ)
             for w in range(48):
                 if w_slot.get(w) == s - 2:
                     v_wquant(w)
             if (s - O_AQ) % 4 == 3 and 0 <= s - O_AQ < NPAIR:
                 v_aquant((s - O_AQ) // 4)
                 aq_slot[(s - O_AQ) // 4] = s
+            if 0 <= s - OQ < NPAIR:
+                v_quant(s - OQ)
             if NORM_ON_V and (s - O_PV - 1) % 2 == 1 and 0 <= s - O_PV - 1 < NPAIR:
                 norm((s - O_PV - 1) // 2)
             pend = []

@@ -30,11 +30,9 @@ GP_A = True
 NORM_ON_V = False
 PIN = True
 HIDE = 3
-W_PLAN = (1, 2, 1, 1)
+W_PLAN = (2, 1, 1, 1)
 NPAIR = 64
 W_START = 4
-GRP_BUFS = 1
-AQ_LAG = 4
 GP_TAIL = 4
 
 
@@ -158,9 +156,11 @@ def tile_selectivetransformerlayer_pb_kernel(tc, q_rot, k_rot, v, attention_mask
             for i in range(2):
                 nc.vector.scalar_tensor_tensor(out=t[:, i, :], in0=PS[p]["ps_s%d" % i][:], scalar=-scale,
                                                in1=mask_sb[:, qb, :], op0=ALU.mult, op1=ALU.subtract)
-            negm = small.tile([P, 2], F32, tag="negm")
-            nc.vector.tensor_reduce(out=negm[:], in_=t[:], axis=AXIS.X, op=ALU.min)
             PS[p]["t"] = t
+
+        def v_min(p):
+            negm = small.tile([P, 2], F32, tag="negm")
+            nc.vector.tensor_reduce(out=negm[:], in_=PS[p]["t"][:], axis=AXIS.X, op=ALU.min)
             PS[p]["negm"] = negm
 
         def s_exp(p):
@@ -185,12 +185,12 @@ def tile_selectivetransformerlayer_pb_kernel(tc, q_rot, k_rot, v, attention_mask
                 nc.scalar.copy(out=stage[:], in_=ps_t[:])
                 PS[p]["stage"] = stage
             else:
-                grp = work.tile([P, 2, P, 4], BF16, tag="grp_s", bufs=2, align_bytes=64)
+                grp = work.tile([P, 2, P, 4], BF16, tag="grp", align_bytes=64)
                 nc.scalar.copy(out=grp[:], in_=ps_t[:].rearrange("p i t q -> p i q t"))
                 PS[p]["grp"] = grp
 
         def g_regroup(p):
-            grp = work.tile([P, 2, P, 4], BF16, tag="grp", bufs=GRP_BUFS, align_bytes=64)
+            grp = work.tile([P, 2, P, 4], BF16, tag="grp", align_bytes=64)
             nc.gpsimd.tensor_scalar(out=grp[:], in0=PS[p]["stage"][:].rearrange("p i t q -> p i q t"),
                                     scalar1=1.0, scalar2=0.0, op0=ALU.mult, op1=ALU.add)
             PS[p]["grp"] = grp
@@ -251,7 +251,7 @@ def tile_selectivetransformerlayer_pb_kernel(tc, q_rot, k_rot, v, attention_mask
                 nc.scalar.copy(out=astage[:], in_=RS[rr]["ps_a"][:])
                 RS[rr]["astage"] = astage
             else:
-                ag = work.tile([P, 2, P, 4], BF16, tag="ag_s", bufs=2, align_bytes=64)
+                ag = work.tile([P, 2, P, 4], BF16, tag="ag", bufs=2, align_bytes=64)
                 nc.scalar.copy(out=ag[:], in_=RS[rr]["ps_a"][:].rearrange("p i t q -> p i q t"))
                 RS[rr]["ag"] = ag
 
@@ -286,7 +286,7 @@ def tile_selectivetransformerlayer_pb_kernel(tc, q_rot, k_rot, v, attention_mask
                 load_wo(pr + 2)
 
         def s_wcopy(w):
-            wg = work.tile([P, 1024], BF16, tag="wg", bufs=2, align_bytes=64)
+            wg = work.tile([P, 1024], BF16, tag="wg", align_bytes=64)
             nc.scalar.copy(out=wg[:].bitcast(F32).rearrange("p (e u) -> p e u", u=2),
                            in_=WS[w]["ps_w"][:].rearrange("p u e -> p e u"))
             WS[w]["wg"] = wg
@@ -313,7 +313,7 @@ def tile_selectivetransformerlayer_pb_kernel(tc, q_rot, k_rot, v, attention_mask
         OQ = 5 if GP_E else 4
         O_PV = OQ + 1
         O_AT = O_PV + 2
-        O_AQ = O_AT + (AQ_LAG if GP_A else 2)
+        O_AQ = O_AT + (3 if GP_A else 2)
         state = {"w": 0}
         w_slot = {}
         aq_slot = {}
@@ -321,24 +321,10 @@ def tile_selectivetransformerlayer_pb_kernel(tc, q_rot, k_rot, v, attention_mask
         lastb = {}
         fin_list = []
         new_fin = []
-        K_SLOT = {-2: 0, 1: 1, 5: 2, 9: 3}
+        K_SLOT = {-3: 0, 1: 1, 5: 2, 9: 3}
         last = NPAIR + O_AQ + 1
-        s = -2
+        s = -3
         while s < last or groups or fin_list or new_fin or "done" not in lastb:
-            if s == 2:
-                v_prep_copy()
-            if s == 3:
-                v_prep_quant()
-            for w in range(48):
-                if w_slot.get(w) == s - 2:
-                    v_wquant(w)
-            if (s - O_AQ) % 4 == 3 and 0 <= s - O_AQ < NPAIR:
-                v_aquant((s - O_AQ) // 4)
-                aq_slot[(s - O_AQ) // 4] = s
-            if 0 <= s - OQ < NPAIR:
-                v_quant(s - OQ)
-            if NORM_ON_V and (s - O_PV - 1) % 2 == 1 and 0 <= s - O_PV - 1 < NPAIR:
-                norm((s - O_PV - 1) // 2)
             pend = []
             done_tr = 0
             n_misc = 0
@@ -347,20 +333,20 @@ def tile_selectivetransformerlayer_pb_kernel(tc, q_rot, k_rot, v, attention_mask
             if s in K_SLOT:
                 pend.extend(pe_kt_list(K_SLOT[s]))
                 n_misc += 1
-            if s % 2 == 0 and 0 <= (s + 2) // 2 < NUNITS:
-                pend.extend(pe_qt_list((s + 2) // 2))
+            if s % 2 == 1 and 0 <= (s + 3) // 2 < NUNITS:
+                pend.extend(pe_qt_list((s + 3) // 2))
                 n_misc += 1
             if (s - O_AT) % 4 == 3 and 0 <= s - O_AT < NPAIR:
                 pend.extend(pe_at_list((s - O_AT) // 4))
                 n_misc += 1
-            if 0 <= s < NPAIR:
-                PS[s] = {}
+            if 0 <= s + 1 < NPAIR:
+                PS[s + 1] = {}
                 for i in range(2):
-                    pe_score(s, i)
                     for rep in range(HIDE):
                         if done_tr < len(pend):
                             tr_bf(pend[done_tr])
                             done_tr += 1
+                    pe_score(s + 1, i)
             for pair in pend[done_tr:]:
                 tr_bf(pair)
             if s >= W_START:
@@ -395,6 +381,22 @@ def tile_selectivetransformerlayer_pb_kernel(tc, q_rot, k_rot, v, attention_mask
                     lastb["done"] = True
             if 0 <= s < NPAIR:
                 v_front(s)
+            if s == 2:
+                v_prep_copy()
+            if s == 3:
+                v_prep_quant()
+            if 0 <= s - OQ < NPAIR:
+                v_quant(s - OQ)
+            for w in range(48):
+                if w_slot.get(w) == s - 2:
+                    v_wquant(w)
+            if (s - O_AQ) % 4 == 3 and 0 <= s - O_AQ < NPAIR:
+                v_aquant((s - O_AQ) // 4)
+                aq_slot[(s - O_AQ) // 4] = s
+            if NORM_ON_V and (s - O_PV - 1) % 2 == 1 and 0 <= s - O_PV - 1 < NPAIR:
+                norm((s - O_PV - 1) // 2)
+            if 0 <= s < NPAIR:
+                v_min(s)
             todo = fin_list[:]
             fin_list = new_fin
             new_fin = []
@@ -402,8 +404,8 @@ def tile_selectivetransformerlayer_pb_kernel(tc, q_rot, k_rot, v, attention_mask
                 op_finish(item[0], item[1], item[2])
             if s - 1 in K_SLOT:
                 s_kcopy(K_SLOT[s - 1])
-            if s % 2 == 1 and 0 <= (s + 1) // 2 < NUNITS:
-                s_qcopy((s + 1) // 2)
+            if s % 2 == 0 and 0 <= (s + 2) // 2 < NUNITS:
+                s_qcopy((s + 2) // 2)
             for w in range(48):
                 if w_slot.get(w) == s - 1:
                     s_wcopy(w)

@@ -25,15 +25,10 @@ UNITS_PER_QB = 8
 NUNITS = NQB * UNITS_PER_QB
 FLOPS = 2 * H * S * S * D * 2 + 2 * S * C * E
 
-GP_E = True
-GP_A = True
-NORM_ON_V = False
-PIN = True
-HIDE = 3
+HIDE = 2
 W_PLAN = (2, 1, 1, 1)
 NPAIR = 64
 W_START = 4
-GP_TAIL = 4
 
 
 def tile_selectivetransformerlayer_pb_kernel(tc, q_rot, k_rot, v, attention_mask, wo, x, out):
@@ -41,7 +36,7 @@ def tile_selectivetransformerlayer_pb_kernel(tc, q_rot, k_rot, v, attention_mask
     scale = 1.0 / math.sqrt(D)
     q_v = q_rot.rearrange("b h (n p) d -> p n (b h) d", p=P)
     k_v = k_rot.rearrange("b g (n p) d -> p (b g n) d", p=P)
-    v_v = v.rearrange("b g (t p) d -> p (b g t) d", p=P)
+    v_v = v.rearrange("b g (u p e) d -> p (b g u) e d", p=P, e=2)
     m_v = attention_mask.rearrange("a b (n p) k -> p (a b n) k", p=P)
     wo_v = wo.rearrange("(n p) c -> p n c", p=P)
     x_v = x.rearrange("b (n p) e -> p (b n) e", p=P)
@@ -52,12 +47,11 @@ def tile_selectivetransformerlayer_pb_kernel(tc, q_rot, k_rot, v, attention_mask
         work = ctx.enter_context(tc.tile_pool(name="work", bufs=3))
         small = ctx.enter_context(tc.tile_pool(name="small", bufs=12))
         psum = ctx.enter_context(tc.psum_pool(name="psum", bufs=1))
-        if PIN:
-            ctx.enter_context(tc.manual_schedule())
+        ctx.enter_context(tc.manual_schedule())
 
         k_raw = keep.tile([P, HKV * 4, D], BF16)
         mask_sb = keep.tile([P, NQB, S], BF16)
-        v_raw = keep.tile([P, HKV, 4, D], BF16)
+        v_raw = keep.tile([P, HKV * 2, 2, D], BF16)
         q_raws = {}
 
         def load_q_part(qb, c4):
@@ -76,7 +70,7 @@ def tile_selectivetransformerlayer_pb_kernel(tc, q_rot, k_rot, v, attention_mask
         nc.sync.dma_start(out=mask_sb[:, 0:1, :], in_=m_v[:, 0:1, :])
         nc.sync.dma_start(out=k_raw[:, 4:16, :], in_=k_v[:, 4:16, :])
         load_q_part(0, 1)
-        nc.sync.dma_start(out=v_raw[:].rearrange("p g t d -> p (g t) d"), in_=v_v)
+        nc.sync.dma_start(out=v_raw[:], in_=v_v)
         load_q_part(0, 2)
         load_q_part(0, 3)
         nc.sync.dma_start(out=mask_sb[:, 1:4, :], in_=m_v[:, 1:4, :])
@@ -92,7 +86,7 @@ def tile_selectivetransformerlayer_pb_kernel(tc, q_rot, k_rot, v, attention_mask
         def pe_kt_list(g):
             ps_k = psum.tile([P, 4, P], BF16, tag="misc", bufs=2)
             KS[g] = ps_k
-            return [(ps_k[:, i, :], k_raw[:, g * 4 + i, :]) for i in range(4)]
+            return [(ps_k[:, i, :], k_raw[:, g * 4 + i, :], ident_bf[:]) for i in range(4)]
 
         def s_kcopy(g):
             nc.scalar.copy(out=kT[:, g * S:(g + 1) * S], in_=KS[g][:].rearrange("p i k -> p (i k)"))
@@ -102,7 +96,7 @@ def tile_selectivetransformerlayer_pb_kernel(tc, q_rot, k_rot, v, attention_mask
         vscales = keep.tile([P, HKV * D], U8, align_bytes=64)
 
         def v_prep_copy():
-            nc.vector.tensor_copy(out=v_grp[:], in_=v_raw[:].rearrange("p g t d -> p g d t"))
+            nc.vector.tensor_copy(out=v_grp[:], in_=v_raw[:].rearrange("p (g u) e d -> p g d (u e)", u=2))
 
         def v_prep_quant():
             nc.vector.quantize_mx(out=vcodes[:].bitcast(FP8X4), scales=vscales[:],
@@ -129,13 +123,13 @@ def tile_selectivetransformerlayer_pb_kernel(tc, q_rot, k_rot, v, attention_mask
         WS = {}
 
         def tr_bf(pair):
-            nc.tensor.transpose(pair[0], pair[1], ident_bf[:])
+            nc.tensor.transpose(pair[0], pair[1], pair[2])
 
         def pe_qt_list(u):
             qb, a = divmod(u, UNITS_PER_QB)
             ps_q = psum.tile([P, 4, P], BF16, tag="misc", bufs=2)
             US[u] = {"ps_q": ps_q}
-            return [(ps_q[:, j, :], q_raws[qb][:, 4 * a + j, :]) for j in range(4)]
+            return [(ps_q[:, j, :], q_raws[qb][:, 4 * a + j, :], ident_bf[:]) for j in range(4)]
 
         def s_qcopy(u):
             qT = work.tile([P, 4, P], BF16, tag="qT")
@@ -173,33 +167,23 @@ def tile_selectivetransformerlayer_pb_kernel(tc, q_rot, k_rot, v, attention_mask
             PS[p]["rowsum"] = rowsum
 
         def pe_et_list(p):
-            ps_t = psum.tile([P, 2, 4, P], BF16, tag="tr", bufs=2)
+            ps_t = psum.tile([P, 2, 2, P], F32, tag="tr", bufs=2)
             PS[p]["ps_t"] = ps_t
-            e = PS[p]["e"]
-            return [(ps_t[:, i, t4, :], e[:, i, t4 * P:(t4 + 1) * P]) for i in range(2) for t4 in range(4)]
+            e32 = PS[p]["e"][:].rearrange("p i s -> p (i s)").bitcast(F32)
+            return [(ps_t[:, i, u, :], e32[:, (2 * i + u) * P:(2 * i + u + 1) * P], ident_f[:])
+                    for i in range(2) for u in range(2)]
 
         def s_fcopy(p):
-            ps_t = PS[p]["ps_t"]
-            if GP_E and p < NPAIR - GP_TAIL:
-                stage = work.tile([P, 2, 4, P], BF16, tag="stage")
-                nc.scalar.copy(out=stage[:], in_=ps_t[:])
-                PS[p]["stage"] = stage
-            else:
-                grp = work.tile([P, 2, P, 4], BF16, tag="grp", align_bytes=64)
-                nc.scalar.copy(out=grp[:], in_=ps_t[:].rearrange("p i t q -> p i q t"))
-                PS[p]["grp"] = grp
-
-        def g_regroup(p):
-            grp = work.tile([P, 2, P, 4], BF16, tag="grp", align_bytes=64)
-            nc.gpsimd.tensor_scalar(out=grp[:], in0=PS[p]["stage"][:].rearrange("p i t q -> p i q t"),
-                                    scalar1=1.0, scalar2=0.0, op0=ALU.mult, op1=ALU.add)
+            grp = work.tile([P, 8 * P], BF16, tag="grp", align_bytes=64)
+            nc.scalar.copy(out=grp[:].bitcast(F32).rearrange("p (i q u) -> p i q u", i=2, u=2),
+                           in_=PS[p]["ps_t"][:].rearrange("p i u q -> p i q u"))
             PS[p]["grp"] = grp
 
         def v_quant(p):
             ecodes = work.tile([P, 2 * P], U32, tag="ecodes", bufs=4, align_bytes=64)
             escales = work.tile([P, 2 * P], U8, tag="escales", bufs=4, align_bytes=64)
             nc.vector.quantize_mx(out=ecodes[:].bitcast(FP8X4), scales=escales[:],
-                                  in_=PS[p]["grp"][:].rearrange("p i q t -> p (i q t)"))
+                                  in_=PS[p]["grp"][:])
             r = small.tile([P, 2], F32, tag="r")
             nc.vector.reciprocal(out=r[:], in_=PS[p]["rowsum"][:])
             PS[p]["ecodes"] = ecodes
@@ -228,37 +212,21 @@ def tile_selectivetransformerlayer_pb_kernel(tc, q_rot, k_rot, v, attention_mask
             attn2 = RS[rr]["attn2"]
             ps_o = US[u]["ps_o"]
             for j in range(4):
-                uu, hh = divmod(j, 2)
                 r = PS[2 * u + j // 2]["r"]
-                if NORM_ON_V:
-                    nc.vector.tensor_scalar_mul(out=attn2[:, gi, 2 * uu:2 * uu + 2, hh * 64:(hh + 1) * 64],
-                                                in0=ps_o[:, j, :].rearrange("p (pp e) -> p e pp", e=2),
-                                                scalar1=r[:, j % 2:j % 2 + 1])
-                else:
-                    nc.scalar.activation(out=attn2[:, gi, 2 * uu:2 * uu + 2, hh * 64:(hh + 1) * 64],
-                                         in_=ps_o[:, j, :].rearrange("p (pp e) -> p e pp", e=2),
-                                         func=ACTF.Copy, scale=r[:, j % 2:j % 2 + 1])
+                nc.scalar.activation(out=attn2[:, gi, j, :], in_=ps_o[:, j, :],
+                                     func=ACTF.Copy, scale=r[:, j % 2:j % 2 + 1])
 
         def pe_at_list(rr):
-            ps_a = psum.tile([P, 2, 4, P], BF16, tag="misc", bufs=2)
+            ps_a = psum.tile([P, 2, 2, P], F32, tag="misc", bufs=2)
             RS[rr]["ps_a"] = ps_a
-            attn2 = RS[rr]["attn2"]
-            return [(ps_a[:, i, t4, :], attn2[:, i, t4, :]) for i in range(2) for t4 in range(4)]
+            a32 = RS[rr]["attn2"][:].rearrange("p i j d -> p (i j d)").bitcast(F32)
+            return [(ps_a[:, i, u, :], a32[:, (2 * i + u) * P:(2 * i + u + 1) * P], ident_f[:])
+                    for i in range(2) for u in range(2)]
 
         def s_acopy(rr):
-            if GP_A and rr < 14:
-                astage = work.tile([P, 2, 4, P], BF16, tag="astage", bufs=2)
-                nc.scalar.copy(out=astage[:], in_=RS[rr]["ps_a"][:])
-                RS[rr]["astage"] = astage
-            else:
-                ag = work.tile([P, 2, P, 4], BF16, tag="ag", bufs=2, align_bytes=64)
-                nc.scalar.copy(out=ag[:], in_=RS[rr]["ps_a"][:].rearrange("p i t q -> p i q t"))
-                RS[rr]["ag"] = ag
-
-        def g_aregroup(rr):
-            ag = work.tile([P, 2, P, 4], BF16, tag="ag", bufs=2, align_bytes=64)
-            nc.gpsimd.tensor_scalar(out=ag[:], in0=RS[rr]["astage"][:].rearrange("p i t q -> p i q t"),
-                                    scalar1=1.0, scalar2=0.0, op0=ALU.mult, op1=ALU.add)
+            ag = work.tile([P, 8 * P], BF16, tag="ag", bufs=2, align_bytes=64)
+            nc.scalar.copy(out=ag[:].bitcast(F32).rearrange("p (i q u) -> p i q u", i=2, u=2),
+                           in_=RS[rr]["ps_a"][:].rearrange("p i u q -> p i q u"))
             RS[rr]["ag"] = ag
 
         def v_aquant(rr):
@@ -271,7 +239,7 @@ def tile_selectivetransformerlayer_pb_kernel(tc, q_rot, k_rot, v, attention_mask
             lo = k4 * 2 * P
             nc.vector.quantize_mx(out=QS[qb]["acodes"][:, lo:lo + 2 * P].bitcast(FP8X4),
                                   scales=QS[qb]["ascales"][:, lo:lo + 2 * P],
-                                  in_=RS[rr]["ag"][:].rearrange("p i q t -> p (i q t)"))
+                                  in_=RS[rr]["ag"][:])
 
         def pe_w(w):
             pr, g = divmod(w, 8)
@@ -310,10 +278,10 @@ def tile_selectivetransformerlayer_pb_kernel(tc, q_rot, k_rot, v, attention_mask
             nc.vector.tensor_tensor(out=o_sb[:], in0=ps[:], in1=x_sb[:, qb, ec * 512:(ec + 1) * 512], op=ALU.add)
             nc.sync.dma_start(out=out_v[:, qb, ec * 512:(ec + 1) * 512], in_=o_sb[:])
 
-        OQ = 5 if GP_E else 4
+        OQ = 4
         O_PV = OQ + 1
         O_AT = O_PV + 2
-        O_AQ = O_AT + (3 if GP_A else 2)
+        O_AQ = O_AT + 2
         state = {"w": 0}
         w_slot = {}
         aq_slot = {}
@@ -393,8 +361,6 @@ def tile_selectivetransformerlayer_pb_kernel(tc, q_rot, k_rot, v, attention_mask
             if (s - O_AQ) % 4 == 3 and 0 <= s - O_AQ < NPAIR:
                 v_aquant((s - O_AQ) // 4)
                 aq_slot[(s - O_AQ) // 4] = s
-            if NORM_ON_V and (s - O_PV - 1) % 2 == 1 and 0 <= s - O_PV - 1 < NPAIR:
-                norm((s - O_PV - 1) // 2)
             if 0 <= s < NPAIR:
                 v_min(s)
             todo = fin_list[:]
@@ -415,12 +381,8 @@ def tile_selectivetransformerlayer_pb_kernel(tc, q_rot, k_rot, v, attention_mask
                 s_fcopy(s - 3)
             if 0 <= s - 1 < NPAIR:
                 s_exp(s - 1)
-            if (not NORM_ON_V) and (s - O_PV - 1) % 2 == 1 and 0 <= s - O_PV - 1 < NPAIR:
+            if (s - O_PV - 1) % 2 == 1 and 0 <= s - O_PV - 1 < NPAIR:
                 norm((s - O_PV - 1) // 2)
-            if GP_E and 0 <= s - 4 < NPAIR - GP_TAIL:
-                g_regroup(s - 4)
-            if GP_A and (s - O_AT - 2) % 4 == 3 and 0 <= s - O_AT - 2 < NPAIR - 8:
-                g_aregroup((s - O_AT - 2) // 4)
             if s == 0:
                 load_q(1)
             if s == 6:

@@ -25,10 +25,62 @@ UNITS_PER_QB = 8
 NUNITS = NQB * UNITS_PER_QB
 FLOPS = 2 * H * S * S * D * 2 + 2 * S * C * E
 
-HIDE = 2
 W_PLAN = (2, 1, 1, 1)
 NPAIR = 64
 W_START = 4
+PE_MASK_TO = 99
+W_FREE = False
+PE_MASK_FROM = 6
+MT_SLOT = {2: 0, 10: 1, 22: 2, 38: 3}
+S_BUFS = 4
+MISC_BUFS = 3
+PV_TAG = "misc"
+PV_BUFS = 3
+OP_TAG = "op"
+OP_BUFS = 1
+ET_BUFS = 3
+ET_TAG = "misc"
+NMASK = (1, 1)
+EXP_LAG = (1, 1)
+O_ET = 2
+NORM_V = (1, 1, 1, 1)
+FC_V = (0, 0, 0, 0)
+L_FC = 0
+L_QU = 1
+L_PV = 1
+L_NM = 1
+L_AT = 1
+L_AC = 0
+L_AQ = 1
+L_WC = 0
+L_WQ = 2
+L_QC = 0
+Q_AHEAD = 3
+PE_ORDER = ("et", "w", "at", "mask0", "kqt", "score0", "mask1", "pv", "score1", "op")
+OPC = 2
+OPC_LATE = 40
+OPC2 = 4
+SPLIT_S = False
+SB_BUFS = 2
+V_ORDER = ("front0", "front1", "wquant", "max0", "vq", "norm", "quant", "max1", "fin", "aquant", "wcopy", "fcopy")
+S_ORDER = ("exp0", "exp1", "fcopy", "norm", "acopy", "wcopy", "kcopy", "qcopy")
+W_ON_V = (0, 1, 0, 1)
+
+
+def pe_masked(p, i):
+    return PE_MASK_FROM <= p < PE_MASK_TO and NMASK[(2 * p + i) % len(NMASK)] == 1
+
+
+def FCOPY_V(p):
+    return FC_V[p % 4] == 1
+
+
+def norm_on_vector(u):
+    return NORM_V[u % 4] == 1
+
+
+def w_on_vector(w):
+    return W_ON_V[w % 4] == 1
 
 
 def tile_selectivetransformerlayer_pb_kernel(tc, q_rot, k_rot, v, attention_mask, wo, x, out):
@@ -81,15 +133,25 @@ def tile_selectivetransformerlayer_pb_kernel(tc, q_rot, k_rot, v, attention_mask
         make_identity(nc, ident_f[:])
 
         kT = keep.tile([P, HKV * S], BF16)
+        mT = keep.tile([P, NQB, 4, P], F32)
         KS = {}
+        MS = {}
 
         def pe_kt_list(g):
-            ps_k = psum.tile([P, 4, P], BF16, tag="misc", bufs=2)
+            ps_k = psum.tile([P, 4, P], BF16, tag="misc", bufs=MISC_BUFS)
             KS[g] = ps_k
             return [(ps_k[:, i, :], k_raw[:, g * 4 + i, :], ident_bf[:]) for i in range(4)]
 
         def s_kcopy(g):
             nc.scalar.copy(out=kT[:, g * S:(g + 1) * S], in_=KS[g][:].rearrange("p i k -> p (i k)"))
+
+        def pe_mt_list(qb):
+            ps_m = psum.tile([P, 4, P], BF16, tag="misc", bufs=MISC_BUFS)
+            MS[qb] = ps_m
+            return [(ps_m[:, t, :], mask_sb[:, qb, t * P:(t + 1) * P], ident_bf[:]) for t in range(4)]
+
+        def s_mcopy(qb):
+            nc.scalar.activation(out=mT[:, qb, :, :], in_=MS[qb][:], func=ACTF.Copy, scale=math.sqrt(D))
 
         v_grp = keep.tile([P, HKV, D, 4], BF16, align_bytes=64)
         vcodes = keep.tile([P, HKV * D], U32, align_bytes=64)
@@ -122,12 +184,12 @@ def tile_selectivetransformerlayer_pb_kernel(tc, q_rot, k_rot, v, attention_mask
         QS = {0: {}, 1: {}, 2: {}, 3: {}}
         WS = {}
 
-        def tr_bf(pair):
-            nc.tensor.transpose(pair[0], pair[1], pair[2])
+        def tr(triple):
+            nc.tensor.transpose(triple[0], triple[1], triple[2])
 
         def pe_qt_list(u):
             qb, a = divmod(u, UNITS_PER_QB)
-            ps_q = psum.tile([P, 4, P], BF16, tag="misc", bufs=2)
+            ps_q = psum.tile([P, 4, P], BF16, tag="misc", bufs=MISC_BUFS)
             US[u] = {"ps_q": ps_q}
             return [(ps_q[:, j, :], q_raws[qb][:, 4 * a + j, :], ident_bf[:]) for j in range(4)]
 
@@ -136,38 +198,56 @@ def tile_selectivetransformerlayer_pb_kernel(tc, q_rot, k_rot, v, attention_mask
             nc.scalar.copy(out=qT[:], in_=US[u]["ps_q"][:])
             US[u]["qT"] = qT
 
+        def pe_mask(p, i):
+            if SPLIT_S and pe_masked(p, i) or not SPLIT_S:
+                ps_s = psum.tile([P, S], F32, tag="s", bufs=S_BUFS)
+            else:
+                ps_s = psum.tile([P, S], F32, tag="sb", bufs=SB_BUFS)
+            PS[p]["ps_s%d" % i] = ps_s
+            if pe_masked(p, i):
+                for t in range(4):
+                    nc.tensor.matmul(out=ps_s[:, t * P:(t + 1) * P], lhsT=mT[:, p // 16, t, :], rhs=ident_f[:],
+                                     start=(t == 0), stop=False, is_transpose=True)
+
         def pe_score(p, i):
             u = p // 2
             g = (u % UNITS_PER_QB) // 2
-            ps_s = psum.tile([P, S], F32, tag="s", bufs=2)
-            nc.tensor.matmul(out=ps_s[:], lhsT=US[u]["qT"][:, 2 * (p % 2) + i, :], rhs=kT[:, g * S:(g + 1) * S],
-                             start=True, stop=True)
-            PS[p]["ps_s%d" % i] = ps_s
+            nc.tensor.matmul(out=PS[p]["ps_s%d" % i][:], lhsT=US[u]["qT"][:, 2 * (p % 2) + i, :],
+                             rhs=kT[:, g * S:(g + 1) * S], start=not pe_masked(p, i), stop=True)
 
-        def v_front(p):
-            qb = p // 16
-            t = work.tile([P, 2, S], F32, tag="t")
-            for i in range(2):
-                nc.vector.scalar_tensor_tensor(out=t[:, i, :], in0=PS[p]["ps_s%d" % i][:], scalar=-scale,
-                                               in1=mask_sb[:, qb, :], op0=ALU.mult, op1=ALU.subtract)
-            PS[p]["t"] = t
+        def v_front(p, i):
+            if pe_masked(p, i):
+                return
+            t = work.tile([P, S], F32, tag="t")
+            nc.vector.scalar_tensor_tensor(out=t[:], in0=PS[p]["ps_s%d" % i][:], scalar=scale,
+                                           in1=mask_sb[:, p // 16, :], op0=ALU.mult, op1=ALU.add)
+            PS[p]["t%d" % i] = t
 
-        def v_min(p):
-            negm = small.tile([P, 2], F32, tag="negm")
-            nc.vector.tensor_reduce(out=negm[:], in_=PS[p]["t"][:], axis=AXIS.X, op=ALU.min)
-            PS[p]["negm"] = negm
+        def v_max(p, i):
+            negm = small.tile([P, 1], F32, tag="negm")
+            PS[p]["negm%d" % i] = negm
+            if pe_masked(p, i):
+                rmax = small.tile([P, 1], F32, tag="rmax")
+                nc.vector.tensor_reduce(out=rmax[:], in_=PS[p]["ps_s%d" % i][:], axis=AXIS.X, op=ALU.max)
+                nc.gpsimd.tensor_scalar(out=negm[:], in0=rmax[:], scalar1=-scale, scalar2=0.0,
+                                        op0=ALU.mult, op1=ALU.add)
+            else:
+                nc.vector.tensor_reduce(out=negm[:], in_=PS[p]["t%d" % i][:], axis=AXIS.X, op=ALU.max, negate=True)
 
-        def s_exp(p):
-            e = work.tile([P, 2, S], BF16, tag="e")
-            rowsum = small.tile([P, 2], F32, tag="rowsum")
-            for i in range(2):
-                nc.scalar.activation(out=e[:, i, :], in_=PS[p]["t"][:, i, :], func=ACTF.Exp,
-                                     bias=PS[p]["negm"][:, i:i + 1], scale=-1.0, accum_out=rowsum[:, i:i + 1])
-            PS[p]["e"] = e
-            PS[p]["rowsum"] = rowsum
+        def s_exp(p, i):
+            if "e" not in PS[p]:
+                e = work.tile([P, 2, S], BF16, tag="e")
+                PS[p]["e"] = e
+                if p % 2 == 0:
+                    rowsum = small.tile([P, 4], F32, tag="rowsum")
+                    US[p // 2]["rowsum"] = rowsum
+            src = PS[p]["ps_s%d" % i] if pe_masked(p, i) else PS[p]["t%d" % i]
+            nc.scalar.activation(out=PS[p]["e"][:, i, :], in_=src[:], func=ACTF.Exp,
+                                 bias=PS[p]["negm%d" % i][:], scale=scale if pe_masked(p, i) else 1.0,
+                                 accum_out=US[p // 2]["rowsum"][:, 2 * (p % 2) + i:2 * (p % 2) + i + 1])
 
         def pe_et_list(p):
-            ps_t = psum.tile([P, 2, 2, P], F32, tag="tr", bufs=2)
+            ps_t = psum.tile([P, 2, 2, P], F32, tag=ET_TAG, bufs=ET_BUFS)
             PS[p]["ps_t"] = ps_t
             e32 = PS[p]["e"][:].rearrange("p i s -> p (i s)").bitcast(F32)
             return [(ps_t[:, i, u, :], e32[:, (2 * i + u) * P:(2 * i + u + 1) * P], ident_f[:])
@@ -175,7 +255,7 @@ def tile_selectivetransformerlayer_pb_kernel(tc, q_rot, k_rot, v, attention_mask
 
         def s_fcopy(p):
             grp = work.tile([P, 8 * P], BF16, tag="grp", align_bytes=64)
-            nc.scalar.copy(out=grp[:].bitcast(F32).rearrange("p (i q u) -> p i q u", i=2, u=2),
+            (nc.vector.tensor_copy if FCOPY_V(p) else nc.scalar.copy)(out=grp[:].bitcast(F32).rearrange("p (i q u) -> p i q u", i=2, u=2),
                            in_=PS[p]["ps_t"][:].rearrange("p i u q -> p i q u"))
             PS[p]["grp"] = grp
 
@@ -184,15 +264,16 @@ def tile_selectivetransformerlayer_pb_kernel(tc, q_rot, k_rot, v, attention_mask
             escales = work.tile([P, 2 * P], U8, tag="escales", bufs=4, align_bytes=64)
             nc.vector.quantize_mx(out=ecodes[:].bitcast(FP8X4), scales=escales[:],
                                   in_=PS[p]["grp"][:])
-            r = small.tile([P, 2], F32, tag="r")
-            nc.vector.reciprocal(out=r[:], in_=PS[p]["rowsum"][:])
             PS[p]["ecodes"] = ecodes
             PS[p]["escales"] = escales
-            PS[p]["r"] = r
+            if p % 2 == 1:
+                r = small.tile([P, 4], F32, tag="r")
+                nc.vector.reciprocal(out=r[:], in_=US[p // 2]["rowsum"][:])
+                US[p // 2]["r"] = r
 
         def pe_pv(u):
             g = (u % UNITS_PER_QB) // 2
-            ps_o = psum.tile([P, 4, P], F32, tag="o")
+            ps_o = psum.tile([P, 4, P], F32, tag=PV_TAG, bufs=PV_BUFS)
             for j in range(4):
                 p, i = 2 * u + j // 2, j % 2
                 nc.tensor.matmul_mx(out=ps_o[:, j, :],
@@ -211,13 +292,17 @@ def tile_selectivetransformerlayer_pb_kernel(tc, q_rot, k_rot, v, attention_mask
                 RS[rr] = {"attn2": attn2}
             attn2 = RS[rr]["attn2"]
             ps_o = US[u]["ps_o"]
-            for j in range(4):
-                r = PS[2 * u + j // 2]["r"]
-                nc.scalar.activation(out=attn2[:, gi, j, :], in_=ps_o[:, j, :],
-                                     func=ACTF.Copy, scale=r[:, j % 2:j % 2 + 1])
+            r = US[u]["r"]
+            if norm_on_vector(u):
+                nc.vector.tensor_tensor(out=attn2[:, gi, :, :], in0=ps_o[:],
+                                        in1=r[:].unsqueeze(2).to_broadcast([P, 4, P]), op=ALU.mult)
+            else:
+                for j in range(4):
+                    nc.scalar.activation(out=attn2[:, gi, j, :], in_=ps_o[:, j, :],
+                                         func=ACTF.Copy, scale=r[:, j:j + 1])
 
         def pe_at_list(rr):
-            ps_a = psum.tile([P, 2, 2, P], F32, tag="misc", bufs=2)
+            ps_a = psum.tile([P, 2, 2, P], F32, tag="misc", bufs=MISC_BUFS)
             RS[rr]["ps_a"] = ps_a
             a32 = RS[rr]["attn2"][:].rearrange("p i j d -> p (i j d)").bitcast(F32)
             return [(ps_a[:, i, u, :], a32[:, (2 * i + u) * P:(2 * i + u + 1) * P], ident_f[:])
@@ -243,7 +328,7 @@ def tile_selectivetransformerlayer_pb_kernel(tc, q_rot, k_rot, v, attention_mask
 
         def pe_w(w):
             pr, g = divmod(w, 8)
-            ps_w = psum.tile([P, 2, 2 * P], F32, tag="misc", bufs=2)
+            ps_w = psum.tile([P, 2, 2 * P], F32, tag="misc", bufs=MISC_BUFS)
             for i in range(2):
                 w32 = wo_raws[pr * 2 + i][:].bitcast(F32)
                 for uu in range(2):
@@ -253,10 +338,14 @@ def tile_selectivetransformerlayer_pb_kernel(tc, q_rot, k_rot, v, attention_mask
             if g == 7 and pr + 2 < 6:
                 load_wo(pr + 2)
 
-        def s_wcopy(w):
+        def w_copy(w):
             wg = work.tile([P, 1024], BF16, tag="wg", align_bytes=64)
-            nc.scalar.copy(out=wg[:].bitcast(F32).rearrange("p (e u) -> p e u", u=2),
-                           in_=WS[w]["ps_w"][:].rearrange("p u e -> p e u"))
+            dst = wg[:].bitcast(F32).rearrange("p (e u) -> p e u", u=2)
+            src = WS[w]["ps_w"][:].rearrange("p u e -> p e u")
+            if w_on_vector(w):
+                nc.vector.tensor_copy(out=dst, in_=src)
+            else:
+                nc.scalar.copy(out=dst, in_=src)
             WS[w]["wg"] = wg
 
         def v_wquant(w):
@@ -278,111 +367,148 @@ def tile_selectivetransformerlayer_pb_kernel(tc, q_rot, k_rot, v, attention_mask
             nc.vector.tensor_tensor(out=o_sb[:], in0=ps[:], in1=x_sb[:, qb, ec * 512:(ec + 1) * 512], op=ALU.add)
             nc.sync.dma_start(out=out_v[:, qb, ec * 512:(ec + 1) * 512], in_=o_sb[:])
 
-        OQ = 4
-        O_PV = OQ + 1
-        O_AT = O_PV + 2
-        O_AQ = O_AT + 2
-        state = {"w": 0}
+        O_FC = O_ET + L_FC
+        O_QU = O_FC + L_QU
+        O_PV = O_QU + L_PV
+        O_NM = O_PV + L_NM
+        O_AT = O_NM + L_AT
+        O_AC = O_AT + L_AC
+        O_AQ = O_AC + L_AQ
+        w_next = 0
         w_slot = {}
         aq_slot = {}
         groups = [(qb, ec) for qb in range(NQB - 1) for ec in range(3)]
         lastb = {}
+        cur = []
         fin_list = []
         new_fin = []
-        K_SLOT = {-3: 0, 1: 1, 5: 2, 9: 3}
+        K_SLOT = {-Q_AHEAD: 0, 0: 1, 4: 2, 8: 3}
         last = NPAIR + O_AQ + 1
-        s = -3
+        s = -Q_AHEAD
         while s < last or groups or fin_list or new_fin or "done" not in lastb:
-            pend = []
-            done_tr = 0
-            n_misc = 0
-            if 0 <= s - 2 < NPAIR:
-                pend.extend(pe_et_list(s - 2))
-            if s in K_SLOT:
-                pend.extend(pe_kt_list(K_SLOT[s]))
-                n_misc += 1
-            if s % 2 == 1 and 0 <= (s + 3) // 2 < NUNITS:
-                pend.extend(pe_qt_list((s + 3) // 2))
-                n_misc += 1
-            if (s - O_AT) % 4 == 3 and 0 <= s - O_AT < NPAIR:
-                pend.extend(pe_at_list((s - O_AT) // 4))
-                n_misc += 1
-            if 0 <= s + 1 < NPAIR:
+            have_next = 0 <= s + 1 < NPAIR
+            if have_next:
                 PS[s + 1] = {}
-                for i in range(2):
-                    for rep in range(HIDE):
-                        if done_tr < len(pend):
-                            tr_bf(pend[done_tr])
-                            done_tr += 1
-                    pe_score(s + 1, i)
-            for pair in pend[done_tr:]:
-                tr_bf(pair)
+            at_now = (s - O_AT) % 4 == 3 and 0 <= s - O_AT < NPAIR
+            qt_now = s % 2 == 1 and 0 <= (s + Q_AHEAD) // 2 < NUNITS
+            n_misc = (s in K_SLOT) + (s in MT_SLOT) + at_now + qt_now
+            w_now = []
             if s >= W_START:
-                for rep in range(min(W_PLAN[s % 4], 2 - n_misc)):
-                    if state["w"] < 48:
-                        pe_w(state["w"])
-                        w_slot[state["w"]] = s
-                        state["w"] += 1
-            if (s - O_PV) % 2 == 1 and 0 <= s - O_PV < NPAIR:
-                pe_pv((s - O_PV) // 2)
-            ready = [gr for gr in groups
-                     if w_slot.get(16 * gr[1] + 15, 999) + 2 < s and aq_slot.get(4 * gr[0] + 3, 999) < s]
-            if ready and not fin_list:
-                qb, ec = ready[0]
-                groups = [gr for gr in groups if gr != (qb, ec)]
-                ps_p = psum.tile([P, 512], F32, tag="op")
-                op_passes(qb, ps_p, ec, 0, 8)
-                new_fin.append((qb, ps_p, ec))
-            if "ps" not in lastb and not groups and not fin_list and not new_fin and s >= NPAIR:
-                ps_l0 = psum.tile([P, 512], F32, tag="op")
-                ps_l1 = psum.tile([P, 512], F32, tag="s", bufs=2)
-                ps_l2 = psum.tile([P, 512], F32, tag="s", bufs=2)
-                lastb["ps"] = [ps_l0, ps_l1, ps_l2]
-                lastb["g"] = 0
-            while "ps" in lastb and lastb["g"] < 8 and aq_slot.get(12 + lastb["g"] // 2, 999) < s:
-                for ec in range(3):
-                    op_passes(NQB - 1, lastb["ps"][ec], ec, lastb["g"], lastb["g"] + 2)
-                    if lastb["g"] == 6:
-                        op_finish(NQB - 1, lastb["ps"][ec], ec)
-                lastb["g"] += 2
-                if lastb["g"] == 8:
-                    lastb["done"] = True
-            if 0 <= s < NPAIR:
-                v_front(s)
-            if s == 2:
-                v_prep_copy()
-            if s == 3:
-                v_prep_quant()
-            if 0 <= s - OQ < NPAIR:
-                v_quant(s - OQ)
-            for w in range(48):
-                if w_slot.get(w) == s - 2:
-                    v_wquant(w)
-            if (s - O_AQ) % 4 == 3 and 0 <= s - O_AQ < NPAIR:
-                v_aquant((s - O_AQ) // 4)
-                aq_slot[(s - O_AQ) // 4] = s
-            if 0 <= s < NPAIR:
-                v_min(s)
-            todo = fin_list[:]
-            fin_list = new_fin
-            new_fin = []
-            for item in todo:
-                op_finish(item[0], item[1], item[2])
-            if s - 1 in K_SLOT:
-                s_kcopy(K_SLOT[s - 1])
-            if s % 2 == 0 and 0 <= (s + 2) // 2 < NUNITS:
-                s_qcopy((s + 2) // 2)
-            for w in range(48):
-                if w_slot.get(w) == s - 1:
-                    s_wcopy(w)
-            if (s - O_AT - 1) % 4 == 3 and 0 <= s - O_AT - 1 < NPAIR:
-                s_acopy((s - O_AT - 1) // 4)
-            if 0 <= s - 3 < NPAIR:
-                s_fcopy(s - 3)
-            if 0 <= s - 1 < NPAIR:
-                s_exp(s - 1)
-            if (s - O_PV - 1) % 2 == 1 and 0 <= s - O_PV - 1 < NPAIR:
-                norm((s - O_PV - 1) // 2)
+                for rep in range(W_PLAN[s % 4] if W_FREE else min(W_PLAN[s % 4], 2 - n_misc)):
+                    if w_next < 48:
+                        w_now.append(w_next)
+                        w_slot[w_next] = s
+                        w_next += 1
+            for step in PE_ORDER:
+                if step == "et" and 0 <= s - O_ET < NPAIR:
+                    for triple in pe_et_list(s - O_ET):
+                        tr(triple)
+                elif step == "kqt":
+                    if s in K_SLOT:
+                        for triple in pe_kt_list(K_SLOT[s]):
+                            tr(triple)
+                    if s in MT_SLOT:
+                        for triple in pe_mt_list(MT_SLOT[s]):
+                            tr(triple)
+                    if qt_now:
+                        for triple in pe_qt_list((s + Q_AHEAD) // 2):
+                            tr(triple)
+                elif step == "w":
+                    for w in w_now:
+                        pe_w(w)
+                elif step == "at" and at_now:
+                    for triple in pe_at_list((s - O_AT) // 4):
+                        tr(triple)
+                elif step in ("mask0", "mask1") and have_next:
+                    pe_mask(s + 1, int(step[4]))
+                elif step in ("score0", "score1") and have_next:
+                    pe_score(s + 1, int(step[5]))
+                elif step == "pv" and (s - O_PV) % 2 == 1 and 0 <= s - O_PV < NPAIR:
+                    pe_pv((s - O_PV) // 2)
+                elif step == "op":
+                    ready = [gr for gr in groups
+                             if w_slot.get(16 * gr[1] + 15, 999) + L_WC + L_WQ < s and aq_slot.get(4 * gr[0] + 3, 999) < s]
+                    if ready and not cur and not fin_list:
+                        cur.append(ready[0])
+                        groups = [gr for gr in groups if gr != cur[0]]
+                        ps_p = psum.tile([P, 512], F32, tag=OP_TAG, bufs=OP_BUFS)
+                        cur.extend([ps_p, 0])
+                    if cur:
+                        hi = min(8, cur[2] + (OPC if s < OPC_LATE else OPC2))
+                        op_passes(cur[0][0], cur[1], cur[0][1], cur[2], hi)
+                        cur[2] = hi
+                        if hi == 8:
+                            new_fin.append((cur[0][0], cur[1], cur[0][1]))
+                            cur.clear()
+                    if "ps" not in lastb and not groups and not cur and not fin_list and not new_fin and s >= NPAIR:
+                        ps_l0 = psum.tile([P, 512], F32, tag="s", bufs=S_BUFS)
+                        ps_l1 = psum.tile([P, 512], F32, tag="s", bufs=S_BUFS)
+                        ps_l2 = psum.tile([P, 512], F32, tag=OP_TAG, bufs=OP_BUFS)
+                        lastb["ps"] = [ps_l0, ps_l1, ps_l2]
+                        lastb["g"] = 0
+                    while "ps" in lastb and lastb["g"] < 8 and aq_slot.get(12 + lastb["g"] // 2, 999) < s:
+                        for ec in range(3):
+                            op_passes(NQB - 1, lastb["ps"][ec], ec, lastb["g"], lastb["g"] + 2)
+                            if lastb["g"] == 6:
+                                op_finish(NQB - 1, lastb["ps"][ec], ec)
+                        lastb["g"] += 2
+                        if lastb["g"] == 8:
+                            lastb["done"] = True
+            for step in V_ORDER:
+                if step in ("front0", "front1") and 0 <= s < NPAIR:
+                    v_front(s, int(step[5]))
+                elif step in ("max0", "max1") and 0 <= s < NPAIR:
+                    v_max(s, int(step[3]))
+                elif step == "vq":
+                    if s == 2:
+                        v_prep_copy()
+                    if s == 3:
+                        v_prep_quant()
+                elif step == "quant" and 0 <= s - O_QU < NPAIR:
+                    v_quant(s - O_QU)
+                elif step == "wcopy":
+                    for w in range(48):
+                        if w_slot.get(w) == s - L_WC and w_on_vector(w):
+                            w_copy(w)
+                elif step == "fcopy" and 0 <= s - O_FC < NPAIR and FCOPY_V(s - O_FC):
+                    s_fcopy(s - O_FC)
+                elif step == "wquant":
+                    for w in range(48):
+                        if w_slot.get(w) == s - L_WC - L_WQ:
+                            v_wquant(w)
+                elif step == "norm" and (s - O_NM) % 2 == 1 and 0 <= s - O_NM < NPAIR and norm_on_vector((s - O_NM) // 2):
+                    norm((s - O_NM) // 2)
+                elif step == "aquant" and (s - O_AQ) % 4 == 3 and 0 <= s - O_AQ < NPAIR:
+                    v_aquant((s - O_AQ) // 4)
+                    aq_slot[(s - O_AQ) // 4] = s
+                elif step == "fin":
+                    todo = fin_list[:]
+                    fin_list = new_fin
+                    new_fin = []
+                    for item in todo:
+                        op_finish(item[0], item[1], item[2])
+            for step in S_ORDER:
+                if step in ("exp0", "exp1"):
+                    i = int(step[3])
+                    if 0 <= s - EXP_LAG[i] < NPAIR:
+                        s_exp(s - EXP_LAG[i], i)
+                elif step == "fcopy" and 0 <= s - O_FC < NPAIR and not FCOPY_V(s - O_FC):
+                    s_fcopy(s - O_FC)
+                elif step == "kcopy":
+                    if s - L_QC in K_SLOT:
+                        s_kcopy(K_SLOT[s - L_QC])
+                    if s - L_QC in MT_SLOT:
+                        s_mcopy(MT_SLOT[s - L_QC])
+                elif step == "wcopy":
+                    for w in range(48):
+                        if w_slot.get(w) == s - L_WC and not w_on_vector(w):
+                            w_copy(w)
+                elif step == "acopy" and (s - O_AC) % 4 == 3 and 0 <= s - O_AC < NPAIR:
+                    s_acopy((s - O_AC) // 4)
+                elif step == "qcopy" and (s - L_QC) % 2 == 1 and 0 <= (s - L_QC + Q_AHEAD) // 2 < NUNITS:
+                    s_qcopy((s - L_QC + Q_AHEAD) // 2)
+                elif step == "norm" and (s - O_NM) % 2 == 1 and 0 <= s - O_NM < NPAIR and not norm_on_vector((s - O_NM) // 2):
+                    norm((s - O_NM) // 2)
             if s == 0:
                 load_q(1)
             if s == 6:

@@ -25,13 +25,20 @@ UNITS_PER_QB = 8
 NUNITS = NQB * UNITS_PER_QB
 FLOPS = 2 * H * S * S * D * 2 + 2 * S * C * E
 
-W_PLAN = (2, 1, 1, 1)
+W_PLAN = (1, 0, 2, 1)
 NPAIR = 64
 W_START = 4
-PE_MASK_TO = 99
-W_FREE = False
-PE_MASK_FROM = 6
-MT_SLOT = {2: 0, 10: 1, 22: 2, 38: 3}
+PE_MASK_TO = 54
+NMASK2 = (0, 1, 1, 1)
+OP_PV = False
+VP_SLOT = 1
+MT0 = 0
+MT_SLOTS = (2, 10, 22, 38)
+LASTB_AT = 60
+LASTS_AT = 64
+WO_FIRST = 2
+W_FREE = True
+PE_MASK_FROM = 2
 S_BUFS = 4
 MISC_BUFS = 3
 PV_TAG = "misc"
@@ -43,7 +50,7 @@ ET_TAG = "misc"
 NMASK = (1, 1)
 EXP_LAG = (1, 1)
 O_ET = 2
-NORM_V = (1, 1, 1, 1)
+NORM_V = (1, 0, 1, 0)
 FC_V = (0, 0, 0, 0)
 L_FC = 0
 L_QU = 1
@@ -51,24 +58,29 @@ L_PV = 1
 L_NM = 1
 L_AT = 1
 L_AC = 0
-L_AQ = 1
+L_AQ = 2
 L_WC = 0
 L_WQ = 2
 L_QC = 0
 Q_AHEAD = 3
-PE_ORDER = ("et", "w", "at", "mask0", "kqt", "score0", "mask1", "pv", "score1", "op")
-OPC = 2
+PE_ORDER = ("et", "at", "kqt", "w", "mask0", "mask1", "score0", "pv", "op", "score1")
+OPC = 1
 OPC_LATE = 40
 OPC2 = 4
+OPC_LATE3 = 58
+OPC3 = 4
 SPLIT_S = False
 SB_BUFS = 2
-V_ORDER = ("front0", "front1", "wquant", "max0", "vq", "norm", "quant", "max1", "fin", "aquant", "wcopy", "fcopy")
-S_ORDER = ("exp0", "exp1", "fcopy", "norm", "acopy", "wcopy", "kcopy", "qcopy")
-W_ON_V = (0, 1, 0, 1)
+V_ORDER = ("front0", "wquant", "front1", "norm", "max0", "fcopy", "max1", "aquant", "vq", "fin", "wcopy", "quant")
+S_ORDER = ("exp0", "exp1", "norm", "fcopy", "kcopy", "wcopy", "qcopy", "acopy")
+W_ON_V = (1, 0, 1, 1)
 
 
 def pe_masked(p, i):
-    return PE_MASK_FROM <= p < PE_MASK_TO and NMASK[(2 * p + i) % len(NMASK)] == 1
+    if p < PE_MASK_FROM:
+        return False
+    pat = NMASK if p < PE_MASK_TO else NMASK2
+    return pat[(2 * p + i) % len(pat)] == 1
 
 
 def FCOPY_V(p):
@@ -116,17 +128,6 @@ def tile_selectivetransformerlayer_pb_kernel(tc, q_rot, k_rot, v, attention_mask
                 for c4 in range(4):
                     load_q_part(qb, c4)
 
-        load_q(0)
-        nc.sync.dma_start(out=k_raw[:, 0:4, :], in_=k_v[:, 0:4, :])
-        load_q_part(0, 0)
-        nc.sync.dma_start(out=mask_sb[:, 0:1, :], in_=m_v[:, 0:1, :])
-        nc.sync.dma_start(out=k_raw[:, 4:16, :], in_=k_v[:, 4:16, :])
-        load_q_part(0, 1)
-        nc.sync.dma_start(out=v_raw[:], in_=v_v)
-        load_q_part(0, 2)
-        load_q_part(0, 3)
-        nc.sync.dma_start(out=mask_sb[:, 1:4, :], in_=m_v[:, 1:4, :])
-
         ident_bf = keep.tile([P, P], BF16)
         make_identity(nc, ident_bf[:])
         ident_f = keep.tile([P, P], F32)
@@ -158,7 +159,9 @@ def tile_selectivetransformerlayer_pb_kernel(tc, q_rot, k_rot, v, attention_mask
         vscales = keep.tile([P, HKV * D], U8, align_bytes=64)
 
         def v_prep_copy():
-            nc.vector.tensor_copy(out=v_grp[:], in_=v_raw[:].rearrange("p (g u) e d -> p g d (u e)", u=2))
+            for g in range(HKV):
+                nc.gpsimd.tensor_scalar(out=v_grp[:, g, :, :], in0=v_raw[:, 2 * g:2 * g + 2, :, :].rearrange("p u e d -> p d (u e)"),
+                                        scalar1=1.0, scalar2=0.0, op0=ALU.mult, op1=ALU.add)
 
         def v_prep_quant():
             nc.vector.quantize_mx(out=vcodes[:].bitcast(FP8X4), scales=vscales[:],
@@ -175,7 +178,22 @@ def tile_selectivetransformerlayer_pb_kernel(tc, q_rot, k_rot, v, attention_mask
                 nc.sync.dma_start(out=wo_raw[:], in_=wo_v[:, pr * 2 + i, :])
                 wo_raws[pr * 2 + i] = wo_raw
 
-        load_wo(0)
+        load_q(0)
+        nc.sync.dma_start(out=k_raw[:, 0:4, :], in_=k_v[:, 0:4, :])
+        load_q_part(0, 0)
+        nc.sync.dma_start(out=mask_sb[:, 0:1, :], in_=m_v[:, 0:1, :])
+        if WO_FIRST == 1:
+            load_wo(0)
+        nc.sync.dma_start(out=k_raw[:, 4:16, :], in_=k_v[:, 4:16, :])
+        load_q_part(0, 1)
+        nc.sync.dma_start(out=v_raw[:], in_=v_v)
+        if WO_FIRST == 2:
+            load_wo(0)
+        load_q_part(0, 2)
+        load_q_part(0, 3)
+        nc.sync.dma_start(out=mask_sb[:, 1:4, :], in_=m_v[:, 1:4, :])
+        if WO_FIRST == 0:
+            load_wo(0)
         load_wo(1)
 
         PS = {}
@@ -379,13 +397,15 @@ def tile_selectivetransformerlayer_pb_kernel(tc, q_rot, k_rot, v, attention_mask
         aq_slot = {}
         groups = [(qb, ec) for qb in range(NQB - 1) for ec in range(3)]
         lastb = {}
+        n_last = 0
         cur = []
         fin_list = []
         new_fin = []
+        MT_SLOT = {MT0: 0, MT_SLOTS[1]: 1, MT_SLOTS[2]: 2, MT_SLOTS[3]: 3}
         K_SLOT = {-Q_AHEAD: 0, 0: 1, 4: 2, 8: 3}
         last = NPAIR + O_AQ + 1
         s = -Q_AHEAD
-        while s < last or groups or fin_list or new_fin or "done" not in lastb:
+        while s < last or groups or fin_list or new_fin or n_last < 3:
             have_next = 0 <= s + 1 < NPAIR
             if have_next:
                 PS[s + 1] = {}
@@ -425,7 +445,7 @@ def tile_selectivetransformerlayer_pb_kernel(tc, q_rot, k_rot, v, attention_mask
                     pe_score(s + 1, int(step[5]))
                 elif step == "pv" and (s - O_PV) % 2 == 1 and 0 <= s - O_PV < NPAIR:
                     pe_pv((s - O_PV) // 2)
-                elif step == "op":
+                elif step == "op" and (not OP_PV or (s - O_PV) % 2 == 1 or s >= NPAIR):
                     ready = [gr for gr in groups
                              if w_slot.get(16 * gr[1] + 15, 999) + L_WC + L_WQ < s and aq_slot.get(4 * gr[0] + 3, 999) < s]
                     if ready and not cur and not fin_list:
@@ -434,35 +454,39 @@ def tile_selectivetransformerlayer_pb_kernel(tc, q_rot, k_rot, v, attention_mask
                         ps_p = psum.tile([P, 512], F32, tag=OP_TAG, bufs=OP_BUFS)
                         cur.extend([ps_p, 0])
                     if cur:
-                        hi = min(8, cur[2] + (OPC if s < OPC_LATE else OPC2))
+                        hi = min(8, cur[2] + (OPC if s < OPC_LATE else OPC2 if s < OPC_LATE3 else OPC3))
                         op_passes(cur[0][0], cur[1], cur[0][1], cur[2], hi)
                         cur[2] = hi
                         if hi == 8:
                             new_fin.append((cur[0][0], cur[1], cur[0][1]))
                             cur.clear()
-                    if "ps" not in lastb and not groups and not cur and not fin_list and not new_fin and s >= NPAIR:
-                        ps_l0 = psum.tile([P, 512], F32, tag="s", bufs=S_BUFS)
-                        ps_l1 = psum.tile([P, 512], F32, tag="s", bufs=S_BUFS)
-                        ps_l2 = psum.tile([P, 512], F32, tag=OP_TAG, bufs=OP_BUFS)
-                        lastb["ps"] = [ps_l0, ps_l1, ps_l2]
-                        lastb["g"] = 0
-                    while "ps" in lastb and lastb["g"] < 8 and aq_slot.get(12 + lastb["g"] // 2, 999) < s:
-                        for ec in range(3):
-                            op_passes(NQB - 1, lastb["ps"][ec], ec, lastb["g"], lastb["g"] + 2)
-                            if lastb["g"] == 6:
-                                op_finish(NQB - 1, lastb["ps"][ec], ec)
-                        lastb["g"] += 2
-                        if lastb["g"] == 8:
-                            lastb["done"] = True
+                    if not groups and not cur and not fin_list and not new_fin:
+                        if 0 not in lastb and s >= LASTB_AT:
+                            ps_l0 = psum.tile([P, 512], F32, tag=OP_TAG, bufs=OP_BUFS)
+                            lastb[0] = [ps_l0, 0]
+                        if 1 not in lastb and s >= LASTS_AT:
+                            ps_l1 = psum.tile([P, 512], F32, tag="s", bufs=S_BUFS)
+                            lastb[1] = [ps_l1, 0]
+                        if 2 not in lastb and s >= LASTS_AT:
+                            ps_l2 = psum.tile([P, 512], F32, tag="s", bufs=S_BUFS)
+                            lastb[2] = [ps_l2, 0]
+                    for ec in lastb:
+                        while lastb[ec][1] < 8 and aq_slot.get(12 + lastb[ec][1] // 2, 999) < s:
+                            g = lastb[ec][1]
+                            op_passes(NQB - 1, lastb[ec][0], ec, g, g + 2)
+                            lastb[ec][1] = g + 2
+                            if g == 6:
+                                op_finish(NQB - 1, lastb[ec][0], ec)
+                                n_last += 1
             for step in V_ORDER:
                 if step in ("front0", "front1") and 0 <= s < NPAIR:
                     v_front(s, int(step[5]))
                 elif step in ("max0", "max1") and 0 <= s < NPAIR:
                     v_max(s, int(step[3]))
                 elif step == "vq":
-                    if s == 2:
+                    if s == VP_SLOT:
                         v_prep_copy()
-                    if s == 3:
+                    if s == VP_SLOT + 1:
                         v_prep_quant()
                 elif step == "quant" and 0 <= s - O_QU < NPAIR:
                     v_quant(s - O_QU)

@@ -25,18 +25,22 @@ UNITS_PER_QB = 8
 NUNITS = NQB * UNITS_PER_QB
 FLOPS = 2 * H * S * S * D * 2 + 2 * S * C * E
 
-W_PLAN = (1, 0, 2, 1)
+W_PLAN = (1, 1, 1, 1)
 NPAIR = 64
-W_START = 4
-PE_MASK_TO = 54
+W_START = 2
+PE_MASK_TO = 34
 NMASK2 = (0, 1, 1, 1)
-OP_PV = False
-VP_SLOT = 1
-MT0 = 0
+OP_PV = True
+VP_SLOT = 2
+MT0 = -1
 MT_SLOTS = (2, 10, 22, 38)
 LASTB_AT = 60
-LASTS_AT = 64
-WO_FIRST = 2
+W_TYPE = (0,)
+W_T2_FROM = 6
+W_TYPE2 = (0,)
+WT_BUFS = 4
+LASTS_AT = 62
+WO_FIRST = 1
 W_FREE = True
 PE_MASK_FROM = 2
 S_BUFS = 4
@@ -50,30 +54,32 @@ ET_TAG = "misc"
 NMASK = (1, 1)
 EXP_LAG = (1, 1)
 O_ET = 2
-NORM_V = (1, 0, 1, 0)
+NORM_V = (1, 1, 1, 1)
 FC_V = (0, 0, 0, 0)
 L_FC = 0
 L_QU = 1
 L_PV = 1
 L_NM = 1
-L_AT = 1
+L_AT = 2
 L_AC = 0
-L_AQ = 2
+L_AQ = 1
 L_WC = 0
-L_WQ = 2
+L_WQ = 1
 L_QC = 0
 Q_AHEAD = 3
-PE_ORDER = ("et", "at", "kqt", "w", "mask0", "mask1", "score0", "pv", "op", "score1")
-OPC = 1
+QN = 8
+WARM = 0
+PE_ORDER = ("et", "w", "at", "mask0", "kqt", "score0", "op", "pv", "mask1", "score1")
+OPC = 2
 OPC_LATE = 40
 OPC2 = 4
-OPC_LATE3 = 58
+OPC_LATE3 = 54
 OPC3 = 4
 SPLIT_S = False
 SB_BUFS = 2
-V_ORDER = ("front0", "wquant", "front1", "norm", "max0", "fcopy", "max1", "aquant", "vq", "fin", "wcopy", "quant")
-S_ORDER = ("exp0", "exp1", "norm", "fcopy", "kcopy", "wcopy", "qcopy", "acopy")
-W_ON_V = (1, 0, 1, 1)
+V_ORDER = ("fin", "vq", "front0", "norm", "front1", "fcopy", "max0", "max1", "aquant", "wcopy", "wquant", "quant")
+S_ORDER = ("exp0", "exp1", "fcopy", "wcopy", "acopy", "qcopy", "norm", "kcopy")
+W_ON_V = (1, 0, 1, 0)
 
 
 def pe_masked(p, i):
@@ -92,7 +98,12 @@ def norm_on_vector(u):
 
 
 def w_on_vector(w):
-    return W_ON_V[w % 4] == 1
+    return w_dve(w // 2) or W_ON_V[w // 2 % 4] == 1
+
+
+def w_dve(j):
+    pat = W_TYPE if j < W_T2_FROM else W_TYPE2
+    return pat[j % len(pat)] == 1
 
 
 def tile_selectivetransformerlayer_pb_kernel(tc, q_rot, k_rot, v, attention_mask, wo, x, out):
@@ -134,6 +145,12 @@ def tile_selectivetransformerlayer_pb_kernel(tc, q_rot, k_rot, v, attention_mask
         make_identity(nc, ident_f[:])
 
         kT = keep.tile([P, HKV * S], BF16)
+        if WARM > 0:
+            zeros = keep.tile([P, S], BF16)
+            nc.vector.memset(zeros[:], 0.0)
+            ps_z = psum.tile([P, 512], F32, tag=OP_TAG, bufs=OP_BUFS)
+            for rep in range(WARM):
+                nc.tensor.matmul(out=ps_z[:], lhsT=zeros[:, 0:P], rhs=zeros[:], start=True, stop=True)
         mT = keep.tile([P, NQB, 4, P], F32)
         KS = {}
         MS = {}
@@ -167,20 +184,37 @@ def tile_selectivetransformerlayer_pb_kernel(tc, q_rot, k_rot, v, attention_mask
             nc.vector.quantize_mx(out=vcodes[:].bitcast(FP8X4), scales=vscales[:],
                                   in_=v_grp[:].rearrange("p g d t -> p (g d t)"))
 
+        wo_x = wo.rearrange("(ec fb n) (g u pb i) -> ec g u pb n fb i", ec=3, n=16, g=8, u=2, pb=4)
+
+        def load_wt(j):
+            ec, g = divmod(j, 8)
+            wt_raw = work.tile([P, 2048], BF16, tag="wt_raw" if w_dve(j) else "wp_raw", bufs=WT_BUFS, align_bytes=64)
+            wo_raws[j] = wt_raw
+            if not w_dve(j):
+                nc.sync.dma_start(out=wt_raw[:].rearrange("p (r c) -> p r c", r=4),
+                                  in_=wo_v[:, 4 * ec:4 * ec + 4, g * 512:(g + 1) * 512])
+                return
+            for pb in range(4):
+                for u in range(2):
+                    nc.sync.dma_start(out=wt_raw[32 * pb + u:32 * pb + 32:2, :].rearrange("p (fb i) -> p fb i", i=64),
+                                      in_=wo_x[ec, g, u, pb])
+
         wcodes = keep.tile([P, 8, E], U32, align_bytes=64)
         wscales = keep.tile([P, 8, E], U8, align_bytes=64)
         x_sb = keep.tile([P, NQB, E], BF16)
         wo_raws = {}
 
         def load_wo(pr):
-            for i in range(2):
-                wo_raw = work.tile([P, C], BF16, tag="wo_raw", bufs=4)
-                nc.sync.dma_start(out=wo_raw[:], in_=wo_v[:, pr * 2 + i, :])
-                wo_raws[pr * 2 + i] = wo_raw
+            if pr < WT_BUFS:
+                for kind in (0, 1):
+                    mine = [n for n in range(24) if w_dve(n) == (kind == 1)]
+                    if pr < len(mine):
+                        load_wt(mine[pr])
 
         load_q(0)
         nc.sync.dma_start(out=k_raw[:, 0:4, :], in_=k_v[:, 0:4, :])
-        load_q_part(0, 0)
+        for c in range(0, 8, 4):
+            nc.sync.dma_start(out=q_raws[0][:, c:c + 4, :], in_=q_v[:, 0, c:c + 4, :])
         nc.sync.dma_start(out=mask_sb[:, 0:1, :], in_=m_v[:, 0:1, :])
         if WO_FIRST == 1:
             load_wo(0)
@@ -194,10 +228,13 @@ def tile_selectivetransformerlayer_pb_kernel(tc, q_rot, k_rot, v, attention_mask
         nc.sync.dma_start(out=mask_sb[:, 1:4, :], in_=m_v[:, 1:4, :])
         if WO_FIRST == 0:
             load_wo(0)
-        load_wo(1)
+        for pr in range(1, WT_BUFS):
+            load_wo(pr)
 
         PS = {}
-        US = {}
+        US = {u: {} for u in range(NUNITS)}
+        QT = {}
+        AS = {}
         RS = {}
         QS = {0: {}, 1: {}, 2: {}, 3: {}}
         WS = {}
@@ -205,16 +242,16 @@ def tile_selectivetransformerlayer_pb_kernel(tc, q_rot, k_rot, v, attention_mask
         def tr(triple):
             nc.tensor.transpose(triple[0], triple[1], triple[2])
 
-        def pe_qt_list(u):
-            qb, a = divmod(u, UNITS_PER_QB)
-            ps_q = psum.tile([P, 4, P], BF16, tag="misc", bufs=MISC_BUFS)
-            US[u] = {"ps_q": ps_q}
-            return [(ps_q[:, j, :], q_raws[qb][:, 4 * a + j, :], ident_bf[:]) for j in range(4)]
+        def pe_qt_list(v):
+            qb, a = divmod(v * QN, 32)
+            ps_q = psum.tile([P, QN, P], BF16, tag="misc", bufs=MISC_BUFS)
+            QT[v] = {"ps_q": ps_q}
+            return [(ps_q[:, j, :], q_raws[qb][:, a + j, :], ident_bf[:]) for j in range(QN)]
 
-        def s_qcopy(u):
-            qT = work.tile([P, 4, P], BF16, tag="qT")
-            nc.scalar.copy(out=qT[:], in_=US[u]["ps_q"][:])
-            US[u]["qT"] = qT
+        def s_qcopy(v):
+            qT = work.tile([P, QN, P], BF16, tag="qT")
+            nc.scalar.copy(out=qT[:], in_=QT[v]["ps_q"][:])
+            QT[v]["qT"] = qT
 
         def pe_mask(p, i):
             if SPLIT_S and pe_masked(p, i) or not SPLIT_S:
@@ -230,7 +267,7 @@ def tile_selectivetransformerlayer_pb_kernel(tc, q_rot, k_rot, v, attention_mask
         def pe_score(p, i):
             u = p // 2
             g = (u % UNITS_PER_QB) // 2
-            nc.tensor.matmul(out=PS[p]["ps_s%d" % i][:], lhsT=US[u]["qT"][:, 2 * (p % 2) + i, :],
+            nc.tensor.matmul(out=PS[p]["ps_s%d" % i][:], lhsT=QT[(2 * p + i) // QN]["qT"][:, (2 * p + i) % QN, :],
                              rhs=kT[:, g * S:(g + 1) * S], start=not pe_masked(p, i), stop=True)
 
         def v_front(p, i):
@@ -311,53 +348,75 @@ def tile_selectivetransformerlayer_pb_kernel(tc, q_rot, k_rot, v, attention_mask
             attn2 = RS[rr]["attn2"]
             ps_o = US[u]["ps_o"]
             r = US[u]["r"]
-            if norm_on_vector(u):
-                nc.vector.tensor_tensor(out=attn2[:, gi, :, :], in0=ps_o[:],
-                                        in1=r[:].unsqueeze(2).to_broadcast([P, 4, P]), op=ALU.mult)
-            else:
-                for j in range(4):
+            nv = 4 if norm_on_vector(u) else 0
+            if u == NUNITS - 1:
+                nv = 2
+            if nv > 0:
+                nc.vector.tensor_tensor(out=attn2[:, gi, 0:nv, :], in0=ps_o[:, 0:nv, :],
+                                        in1=r[:, 0:nv].unsqueeze(2).to_broadcast([P, nv, P]), op=ALU.mult)
+            if nv < 4:
+                for j in range(nv, 4):
                     nc.scalar.activation(out=attn2[:, gi, j, :], in_=ps_o[:, j, :],
                                          func=ACTF.Copy, scale=r[:, j:j + 1])
 
-        def pe_at_list(rr):
+        def piece(d):
+            if d < 0:
+                return None
+            if d >= NPAIR - 4:
+                return {NPAIR - 3: (15, 0, 1), NPAIR - 1: (15, 1, 2)}.get(d)
+            return (d // 4, 0, 2) if d % 4 == 3 else None
+
+        def pe_at_list(pc):
+            rr, lo, hi = pc
             ps_a = psum.tile([P, 2, 2, P], F32, tag="misc", bufs=MISC_BUFS)
-            RS[rr]["ps_a"] = ps_a
+            AS[pc] = {"ps_a": ps_a}
             a32 = RS[rr]["attn2"][:].rearrange("p i j d -> p (i j d)").bitcast(F32)
             return [(ps_a[:, i, u, :], a32[:, (2 * i + u) * P:(2 * i + u + 1) * P], ident_f[:])
-                    for i in range(2) for u in range(2)]
+                    for i in range(lo, hi) for u in range(2)]
 
-        def s_acopy(rr):
-            ag = work.tile([P, 8 * P], BF16, tag="ag", bufs=2, align_bytes=64)
-            nc.scalar.copy(out=ag[:].bitcast(F32).rearrange("p (i q u) -> p i q u", i=2, u=2),
-                           in_=RS[rr]["ps_a"][:].rearrange("p i u q -> p i q u"))
-            RS[rr]["ag"] = ag
+        def s_acopy(pc):
+            rr, lo, hi = pc
+            ag = work.tile([P, 2, 4 * P], BF16, tag="ag", bufs=2, align_bytes=64)
+            for_words = ag[:].bitcast(F32).rearrange("p i (q u) -> p i q u", u=2)
+            nc.scalar.copy(out=for_words[:, lo:hi, :, :],
+                           in_=AS[pc]["ps_a"][:, lo:hi, :, :].rearrange("p i u q -> p i q u"))
+            AS[pc]["ag"] = ag
 
-        def v_aquant(rr):
+        def v_aquant(pc):
+            rr, lo, hi = pc
             qb, k4 = divmod(rr, 4)
             if k4 == 0:
                 acodes = work.tile([P, 8 * P], U32, tag="acodes", bufs=4, align_bytes=64)
                 ascales = work.tile([P, 8 * P], U8, tag="ascales", bufs=4, align_bytes=64)
                 QS[qb]["acodes"] = acodes
                 QS[qb]["ascales"] = ascales
-            lo = k4 * 2 * P
-            nc.vector.quantize_mx(out=QS[qb]["acodes"][:, lo:lo + 2 * P].bitcast(FP8X4),
-                                  scales=QS[qb]["ascales"][:, lo:lo + 2 * P],
-                                  in_=RS[rr]["ag"][:])
+            a, b = (k4 * 2 + lo) * P, (k4 * 2 + hi) * P
+            nc.vector.quantize_mx(out=QS[qb]["acodes"][:, a:b].bitcast(FP8X4),
+                                  scales=QS[qb]["ascales"][:, a:b],
+                                  in_=AS[pc]["ag"][:, lo:hi, :].rearrange("p i c -> p (i c)"))
 
         def pe_w(w):
-            pr, g = divmod(w, 8)
-            ps_w = psum.tile([P, 2, 2 * P], F32, tag="misc", bufs=MISC_BUFS)
-            for i in range(2):
-                w32 = wo_raws[pr * 2 + i][:].bitcast(F32)
-                for uu in range(2):
-                    lo = g * 256 + uu * P
-                    nc.tensor.transpose(ps_w[:, uu, i * P:(i + 1) * P], w32[:, lo:lo + P], ident_f[:])
-            WS[w] = {"ps_w": ps_w}
-            if g == 7 and pr + 2 < 6:
-                load_wo(pr + 2)
+            j, half = divmod(w, 2)
+            if not w_dve(j):
+                ps_w = psum.tile([P, 2, 2 * P], F32, tag="misc", bufs=MISC_BUFS)
+                w32 = wo_raws[j][:].bitcast(F32)
+                for i in range(2):
+                    for uu in range(2):
+                        lo = (2 * half + i) * 256 + uu * P
+                        nc.tensor.transpose(ps_w[:, uu, i * P:(i + 1) * P], w32[:, lo:lo + P], ident_f[:])
+                WS[w] = {"ps_w": ps_w}
+            if half == 1:
+                nxt = [n for n in range(j + 1, 24) if w_dve(n) == w_dve(j)]
+                if len(nxt) >= WT_BUFS:
+                    load_wt(nxt[WT_BUFS - 1])
 
         def w_copy(w):
             wg = work.tile([P, 1024], BF16, tag="wg", align_bytes=64)
+            if w_dve(w // 2):
+                nc.vector.transpose(out=wg[:].bitcast(F32),
+                                    in_=wo_raws[w // 2][:, (w % 2) * 1024:(w % 2) * 1024 + 1024].bitcast(F32))
+                WS[w] = {"wg": wg}
+                return
             dst = wg[:].bitcast(F32).rearrange("p (e u) -> p e u", u=2)
             src = WS[w]["ps_w"][:].rearrange("p u e -> p e u")
             if w_on_vector(w):
@@ -367,7 +426,7 @@ def tile_selectivetransformerlayer_pb_kernel(tc, q_rot, k_rot, v, attention_mask
             WS[w]["wg"] = wg
 
         def v_wquant(w):
-            pr, g = divmod(w, 8)
+            pr, g = 2 * (w // 16) + w % 2, w // 2 % 8
             nc.vector.quantize_mx(out=wcodes[:, g, pr * 256:(pr + 1) * 256].bitcast(FP8X4),
                                   scales=wscales[:, g, pr * 256:(pr + 1) * 256], in_=WS[w]["wg"][:])
 
@@ -409,8 +468,8 @@ def tile_selectivetransformerlayer_pb_kernel(tc, q_rot, k_rot, v, attention_mask
             have_next = 0 <= s + 1 < NPAIR
             if have_next:
                 PS[s + 1] = {}
-            at_now = (s - O_AT) % 4 == 3 and 0 <= s - O_AT < NPAIR
-            qt_now = s % 2 == 1 and 0 <= (s + Q_AHEAD) // 2 < NUNITS
+            at_now = piece(s - O_AT) is not None
+            qt_now = (s + Q_AHEAD) % (QN // 2) == 0 and 0 <= (s + Q_AHEAD) // (QN // 2) < 128 // QN
             n_misc = (s in K_SLOT) + (s in MT_SLOT) + at_now + qt_now
             w_now = []
             if s >= W_START:
@@ -431,13 +490,13 @@ def tile_selectivetransformerlayer_pb_kernel(tc, q_rot, k_rot, v, attention_mask
                         for triple in pe_mt_list(MT_SLOT[s]):
                             tr(triple)
                     if qt_now:
-                        for triple in pe_qt_list((s + Q_AHEAD) // 2):
+                        for triple in pe_qt_list((s + Q_AHEAD) // (QN // 2)):
                             tr(triple)
                 elif step == "w":
                     for w in w_now:
                         pe_w(w)
                 elif step == "at" and at_now:
-                    for triple in pe_at_list((s - O_AT) // 4):
+                    for triple in pe_at_list(piece(s - O_AT)):
                         tr(triple)
                 elif step in ("mask0", "mask1") and have_next:
                     pe_mask(s + 1, int(step[4]))
@@ -447,7 +506,7 @@ def tile_selectivetransformerlayer_pb_kernel(tc, q_rot, k_rot, v, attention_mask
                     pe_pv((s - O_PV) // 2)
                 elif step == "op" and (not OP_PV or (s - O_PV) % 2 == 1 or s >= NPAIR):
                     ready = [gr for gr in groups
-                             if w_slot.get(16 * gr[1] + 15, 999) + L_WC + L_WQ < s and aq_slot.get(4 * gr[0] + 3, 999) < s]
+                             if w_slot.get(16 * gr[1] + 15, 999) + L_WC + L_WQ < s and aq_slot.get(8 * gr[0] + 7, 999) < s]
                     if ready and not cur and not fin_list:
                         cur.append(ready[0])
                         groups = [gr for gr in groups if gr != cur[0]]
@@ -471,11 +530,11 @@ def tile_selectivetransformerlayer_pb_kernel(tc, q_rot, k_rot, v, attention_mask
                             ps_l2 = psum.tile([P, 512], F32, tag="s", bufs=S_BUFS)
                             lastb[2] = [ps_l2, 0]
                     for ec in lastb:
-                        while lastb[ec][1] < 8 and aq_slot.get(12 + lastb[ec][1] // 2, 999) < s:
+                        while lastb[ec][1] < 8 and aq_slot.get(24 + lastb[ec][1], 999) < s:
                             g = lastb[ec][1]
-                            op_passes(NQB - 1, lastb[ec][0], ec, g, g + 2)
-                            lastb[ec][1] = g + 2
-                            if g == 6:
+                            op_passes(NQB - 1, lastb[ec][0], ec, g, g + 1)
+                            lastb[ec][1] = g + 1
+                            if g == 7:
                                 op_finish(NQB - 1, lastb[ec][0], ec)
                                 n_last += 1
             for step in V_ORDER:
@@ -502,9 +561,11 @@ def tile_selectivetransformerlayer_pb_kernel(tc, q_rot, k_rot, v, attention_mask
                             v_wquant(w)
                 elif step == "norm" and (s - O_NM) % 2 == 1 and 0 <= s - O_NM < NPAIR and norm_on_vector((s - O_NM) // 2):
                     norm((s - O_NM) // 2)
-                elif step == "aquant" and (s - O_AQ) % 4 == 3 and 0 <= s - O_AQ < NPAIR:
-                    v_aquant((s - O_AQ) // 4)
-                    aq_slot[(s - O_AQ) // 4] = s
+                elif step == "aquant" and piece(s - O_AQ) is not None:
+                    pc = piece(s - O_AQ)
+                    v_aquant(pc)
+                    for i in range(pc[1], pc[2]):
+                        aq_slot[2 * pc[0] + i] = s
                 elif step == "fin":
                     todo = fin_list[:]
                     fin_list = new_fin
@@ -527,10 +588,10 @@ def tile_selectivetransformerlayer_pb_kernel(tc, q_rot, k_rot, v, attention_mask
                     for w in range(48):
                         if w_slot.get(w) == s - L_WC and not w_on_vector(w):
                             w_copy(w)
-                elif step == "acopy" and (s - O_AC) % 4 == 3 and 0 <= s - O_AC < NPAIR:
-                    s_acopy((s - O_AC) // 4)
-                elif step == "qcopy" and (s - L_QC) % 2 == 1 and 0 <= (s - L_QC + Q_AHEAD) // 2 < NUNITS:
-                    s_qcopy((s - L_QC + Q_AHEAD) // 2)
+                elif step == "acopy" and piece(s - O_AC) is not None:
+                    s_acopy(piece(s - O_AC))
+                elif step == "qcopy" and (s - L_QC + Q_AHEAD) % (QN // 2) == 0 and 0 <= (s - L_QC + Q_AHEAD) // (QN // 2) < 128 // QN:
+                    s_qcopy((s - L_QC + Q_AHEAD) // (QN // 2))
                 elif step == "norm" and (s - O_NM) % 2 == 1 and 0 <= s - O_NM < NPAIR and not norm_on_vector((s - O_NM) // 2):
                     norm((s - O_NM) // 2)
             if s == 0:

@@ -25,23 +25,19 @@ UNITS_PER_QB = 8
 NUNITS = NQB * UNITS_PER_QB
 FLOPS = 2 * H * S * S * D * 2 + 2 * S * C * E
 
-W_PLAN = (1, 1, 1, 1)
+W_PLAN = (2, 1, 2, 1)
 NPAIR = 64
-W_START = 2
-PE_MASK_TO = 34
+W_START = 3
+PE_MASK_TO = 42
 NMASK2 = (0, 1, 1, 1)
 OP_PV = True
 VP_SLOT = 2
-MT0 = -1
+MT0 = -2
 MT_SLOTS = (2, 10, 22, 38)
 LASTB_AT = 60
-W_TYPE = (0,)
-W_T2_FROM = 6
-W_TYPE2 = (0,)
-WT_BUFS = 4
-LASTS_AT = 62
-WO_FIRST = 1
-W_FREE = True
+LASTS_AT = 64
+WO_FIRST = 2
+W_FREE = False
 PE_MASK_FROM = 2
 S_BUFS = 4
 MISC_BUFS = 3
@@ -60,26 +56,26 @@ L_FC = 0
 L_QU = 1
 L_PV = 1
 L_NM = 1
-L_AT = 2
+L_AT = 1
 L_AC = 0
-L_AQ = 1
+L_AQ = 2
 L_WC = 0
 L_WQ = 1
 L_QC = 0
 Q_AHEAD = 3
-QN = 8
+QN = 4
 WARM = 0
-PE_ORDER = ("et", "w", "at", "mask0", "kqt", "score0", "op", "pv", "mask1", "score1")
+PE_ORDER = ("et", "w", "at", "kqt", "mask0", "score0", "op", "pv", "mask1", "score1")
 OPC = 2
 OPC_LATE = 40
 OPC2 = 4
-OPC_LATE3 = 54
+OPC_LATE3 = 58
 OPC3 = 4
 SPLIT_S = False
 SB_BUFS = 2
-V_ORDER = ("fin", "vq", "front0", "norm", "front1", "fcopy", "max0", "max1", "aquant", "wcopy", "wquant", "quant")
-S_ORDER = ("exp0", "exp1", "fcopy", "wcopy", "acopy", "qcopy", "norm", "kcopy")
-W_ON_V = (1, 0, 1, 0)
+V_ORDER = ("vq", "front0", "fin", "front1", "norm", "max0", "max1", "fcopy", "aquant", "wcopy", "quant", "wquant")
+S_ORDER = ("exp0", "exp1", "fcopy", "wcopy", "kcopy", "acopy", "norm", "qcopy")
+W_ON_V = (0, 1, 0, 1)
 
 
 def pe_masked(p, i):
@@ -98,12 +94,7 @@ def norm_on_vector(u):
 
 
 def w_on_vector(w):
-    return w_dve(w // 2) or W_ON_V[w // 2 % 4] == 1
-
-
-def w_dve(j):
-    pat = W_TYPE if j < W_T2_FROM else W_TYPE2
-    return pat[j % len(pat)] == 1
+    return W_ON_V[w % 4] == 1
 
 
 def tile_selectivetransformerlayer_pb_kernel(tc, q_rot, k_rot, v, attention_mask, wo, x, out):
@@ -184,32 +175,16 @@ def tile_selectivetransformerlayer_pb_kernel(tc, q_rot, k_rot, v, attention_mask
             nc.vector.quantize_mx(out=vcodes[:].bitcast(FP8X4), scales=vscales[:],
                                   in_=v_grp[:].rearrange("p g d t -> p (g d t)"))
 
-        wo_x = wo.rearrange("(ec fb n) (g u pb i) -> ec g u pb n fb i", ec=3, n=16, g=8, u=2, pb=4)
-
-        def load_wt(j):
-            ec, g = divmod(j, 8)
-            wt_raw = work.tile([P, 2048], BF16, tag="wt_raw" if w_dve(j) else "wp_raw", bufs=WT_BUFS, align_bytes=64)
-            wo_raws[j] = wt_raw
-            if not w_dve(j):
-                nc.sync.dma_start(out=wt_raw[:].rearrange("p (r c) -> p r c", r=4),
-                                  in_=wo_v[:, 4 * ec:4 * ec + 4, g * 512:(g + 1) * 512])
-                return
-            for pb in range(4):
-                for u in range(2):
-                    nc.sync.dma_start(out=wt_raw[32 * pb + u:32 * pb + 32:2, :].rearrange("p (fb i) -> p fb i", i=64),
-                                      in_=wo_x[ec, g, u, pb])
-
         wcodes = keep.tile([P, 8, E], U32, align_bytes=64)
         wscales = keep.tile([P, 8, E], U8, align_bytes=64)
         x_sb = keep.tile([P, NQB, E], BF16)
         wo_raws = {}
 
         def load_wo(pr):
-            if pr < WT_BUFS:
-                for kind in (0, 1):
-                    mine = [n for n in range(24) if w_dve(n) == (kind == 1)]
-                    if pr < len(mine):
-                        load_wt(mine[pr])
+            for i in range(2):
+                wo_raw = work.tile([P, C], BF16, tag="wo_raw", bufs=4)
+                nc.sync.dma_start(out=wo_raw[:], in_=wo_v[:, pr * 2 + i, :])
+                wo_raws[pr * 2 + i] = wo_raw
 
         load_q(0)
         nc.sync.dma_start(out=k_raw[:, 0:4, :], in_=k_v[:, 0:4, :])
@@ -228,8 +203,7 @@ def tile_selectivetransformerlayer_pb_kernel(tc, q_rot, k_rot, v, attention_mask
         nc.sync.dma_start(out=mask_sb[:, 1:4, :], in_=m_v[:, 1:4, :])
         if WO_FIRST == 0:
             load_wo(0)
-        for pr in range(1, WT_BUFS):
-            load_wo(pr)
+        load_wo(1)
 
         PS = {}
         US = {u: {} for u in range(NUNITS)}
@@ -396,27 +370,19 @@ def tile_selectivetransformerlayer_pb_kernel(tc, q_rot, k_rot, v, attention_mask
                                   in_=AS[pc]["ag"][:, lo:hi, :].rearrange("p i c -> p (i c)"))
 
         def pe_w(w):
-            j, half = divmod(w, 2)
-            if not w_dve(j):
-                ps_w = psum.tile([P, 2, 2 * P], F32, tag="misc", bufs=MISC_BUFS)
-                w32 = wo_raws[j][:].bitcast(F32)
-                for i in range(2):
-                    for uu in range(2):
-                        lo = (2 * half + i) * 256 + uu * P
-                        nc.tensor.transpose(ps_w[:, uu, i * P:(i + 1) * P], w32[:, lo:lo + P], ident_f[:])
-                WS[w] = {"ps_w": ps_w}
-            if half == 1:
-                nxt = [n for n in range(j + 1, 24) if w_dve(n) == w_dve(j)]
-                if len(nxt) >= WT_BUFS:
-                    load_wt(nxt[WT_BUFS - 1])
+            pr, g = divmod(w, 8)
+            ps_w = psum.tile([P, 2, 2 * P], F32, tag="misc", bufs=MISC_BUFS)
+            for i in range(2):
+                w32 = wo_raws[pr * 2 + i][:].bitcast(F32)
+                for uu in range(2):
+                    lo = g * 256 + uu * P
+                    nc.tensor.transpose(ps_w[:, uu, i * P:(i + 1) * P], w32[:, lo:lo + P], ident_f[:])
+            WS[w] = {"ps_w": ps_w}
+            if g == 7 and pr + 2 < 6:
+                load_wo(pr + 2)
 
         def w_copy(w):
             wg = work.tile([P, 1024], BF16, tag="wg", align_bytes=64)
-            if w_dve(w // 2):
-                nc.vector.transpose(out=wg[:].bitcast(F32),
-                                    in_=wo_raws[w // 2][:, (w % 2) * 1024:(w % 2) * 1024 + 1024].bitcast(F32))
-                WS[w] = {"wg": wg}
-                return
             dst = wg[:].bitcast(F32).rearrange("p (e u) -> p e u", u=2)
             src = WS[w]["ps_w"][:].rearrange("p u e -> p e u")
             if w_on_vector(w):
@@ -426,7 +392,7 @@ def tile_selectivetransformerlayer_pb_kernel(tc, q_rot, k_rot, v, attention_mask
             WS[w]["wg"] = wg
 
         def v_wquant(w):
-            pr, g = 2 * (w // 16) + w % 2, w // 2 % 8
+            pr, g = divmod(w, 8)
             nc.vector.quantize_mx(out=wcodes[:, g, pr * 256:(pr + 1) * 256].bitcast(FP8X4),
                                   scales=wscales[:, g, pr * 256:(pr + 1) * 256], in_=WS[w]["wg"][:])
 

@@ -166,14 +166,12 @@ def tile_selectivetransformerlayer_pb_kernel(tc, q_rot, k_rot, v, attention_mask
         vcodes = keep.tile([P, HKV * D], U32, align_bytes=64)
         vscales = keep.tile([P, HKV * D], U8, align_bytes=64)
 
-        def v_prep_copy():
-            for g in range(HKV):
-                nc.gpsimd.tensor_scalar(out=v_grp[:, g, :, :], in0=v_raw[:, 2 * g:2 * g + 2, :, :].rearrange("p u e d -> p d (u e)"),
-                                        scalar1=1.0, scalar2=0.0, op0=ALU.mult, op1=ALU.add)
+        def v_prep_copy(g):
+            nc.vector.tensor_copy(out=v_grp[:, g, :, :], in_=v_raw[:, 2 * g:2 * g + 2, :, :].rearrange("p u e d -> p d (u e)"))
 
-        def v_prep_quant():
-            nc.vector.quantize_mx(out=vcodes[:].bitcast(FP8X4), scales=vscales[:],
-                                  in_=v_grp[:].rearrange("p g d t -> p (g d t)"))
+        def v_prep_quant(g):
+            nc.vector.quantize_mx(out=vcodes[:, g * D:(g + 1) * D].bitcast(FP8X4), scales=vscales[:, g * D:(g + 1) * D],
+                                  in_=v_grp[:, g, :, :].rearrange("p d t -> p (d t)"))
 
         wcodes = keep.tile([P, 8, E], U32, align_bytes=64)
         wscales = keep.tile([P, 8, E], U8, align_bytes=64)
@@ -509,10 +507,10 @@ def tile_selectivetransformerlayer_pb_kernel(tc, q_rot, k_rot, v, attention_mask
                 elif step in ("max0", "max1") and 0 <= s < NPAIR:
                     v_max(s, int(step[3]))
                 elif step == "vq":
-                    if s == VP_SLOT:
-                        v_prep_copy()
-                    if s == VP_SLOT + 1:
-                        v_prep_quant()
+                    if (s - VP_SLOT) % 4 == 0 and 0 <= (s - VP_SLOT) // 4 < HKV:
+                        v_prep_copy((s - VP_SLOT) // 4)
+                    if (s - VP_SLOT) % 4 == 1 and 0 <= (s - VP_SLOT) // 4 < HKV:
+                        v_prep_quant((s - VP_SLOT) // 4)
                 elif step == "quant" and 0 <= s - O_QU < NPAIR:
                     v_quant(s - O_QU)
                 elif step == "wcopy":

@@ -38,7 +38,7 @@ LASTB_AT = 60
 LASTS_AT = 64
 WO_FIRST = 2
 W_FREE = False
-PE_MASK_FROM = 2
+PE_MASK_FROM = 1
 S_BUFS = 4
 MISC_BUFS = 3
 PV_TAG = "misc"
@@ -64,6 +64,9 @@ L_WQ = 1
 L_QC = 0
 Q_AHEAD = 3
 QN = 4
+DUM_FROM = 99
+DUM_TO = 99
+DUM_N = 512
 WARM = 0
 PE_ORDER = ("et", "w", "at", "kqt", "mask0", "score0", "op", "pv", "mask1", "score1")
 OPC = 2
@@ -184,22 +187,31 @@ def tile_selectivetransformerlayer_pb_kernel(tc, q_rot, k_rot, v, attention_mask
                 nc.sync.dma_start(out=wo_raw[:], in_=wo_v[:, pr * 2 + i, :])
                 wo_raws[pr * 2 + i] = wo_raw
 
+        def load_k(g):
+            nc.sync.dma_start(out=k_raw[:, 4 * g:4 * g + 4, :], in_=k_v[:, 4 * g:4 * g + 4, :])
+
+        def load_v(g):
+            nc.sync.dma_start(out=v_raw[:, 2 * g:2 * g + 2, :, :], in_=v_v[:, 2 * g:2 * g + 2, :, :])
+
         load_q(0)
-        nc.sync.dma_start(out=k_raw[:, 0:4, :], in_=k_v[:, 0:4, :])
-        for c in range(0, 8, 4):
-            nc.sync.dma_start(out=q_raws[0][:, c:c + 4, :], in_=q_v[:, 0, c:c + 4, :])
+        load_k(0)
+        nc.sync.dma_start(out=q_raws[0][:, 0:4, :], in_=q_v[:, 0, 0:4, :])
         nc.sync.dma_start(out=mask_sb[:, 0:1, :], in_=m_v[:, 0:1, :])
-        if WO_FIRST == 1:
-            load_wo(0)
-        nc.sync.dma_start(out=k_raw[:, 4:16, :], in_=k_v[:, 4:16, :])
+        nc.sync.dma_start(out=q_raws[0][:, 4:8, :], in_=q_v[:, 0, 4:8, :])
+        load_k(1)
+        load_v(0)
         load_q_part(0, 1)
-        nc.sync.dma_start(out=v_raw[:], in_=v_v)
         if WO_FIRST == 2:
             load_wo(0)
+        load_k(2)
+        load_v(1)
         load_q_part(0, 2)
+        load_k(3)
+        load_v(2)
         load_q_part(0, 3)
+        load_v(3)
         nc.sync.dma_start(out=mask_sb[:, 1:4, :], in_=m_v[:, 1:4, :])
-        if WO_FIRST == 0:
+        if WO_FIRST != 2:
             load_wo(0)
         load_wo(1)
 
@@ -456,6 +468,9 @@ def tile_selectivetransformerlayer_pb_kernel(tc, q_rot, k_rot, v, attention_mask
                     if qt_now:
                         for triple in pe_qt_list((s + Q_AHEAD) // (QN // 2)):
                             tr(triple)
+                elif step == "dum" and DUM_FROM <= s < DUM_TO:
+                    ps_d = psum.tile([P, 512], F32, tag=OP_TAG, bufs=OP_BUFS)
+                    nc.tensor.matmul(out=ps_d[:, 0:DUM_N], lhsT=ident_bf[:], rhs=kT[:, 0:DUM_N], start=True, stop=True)
                 elif step == "w":
                     for w in w_now:
                         pe_w(w)

@@ -35,6 +35,8 @@ VP_SLOT = 2
 MT0 = -2
 MT_SLOTS = (2, 10, 22, 38)
 LASTB_AT = 60
+LBN = 1
+LB0 = 1
 LASTS_AT = 64
 WO_FIRST = 2
 W_FREE = False
@@ -67,7 +69,8 @@ QN = 4
 DUM_FROM = 99
 DUM_TO = 99
 DUM_N = 512
-WARM = 0
+WARM = 5
+WO_CUT = 2
 PE_ORDER = ("et", "w", "at", "kqt", "mask0", "score0", "op", "pv", "mask1", "score1")
 OPC = 2
 OPC_LATE = 40
@@ -184,8 +187,11 @@ def tile_selectivetransformerlayer_pb_kernel(tc, q_rot, k_rot, v, attention_mask
         def load_wo(pr):
             for i in range(2):
                 wo_raw = work.tile([P, C], BF16, tag="wo_raw", bufs=4)
-                nc.sync.dma_start(out=wo_raw[:], in_=wo_v[:, pr * 2 + i, :])
                 wo_raws[pr * 2 + i] = wo_raw
+            for lo in range(0, C, C // WO_CUT):
+                for i in range(2):
+                    nc.sync.dma_start(out=wo_raws[pr * 2 + i][:, lo:lo + C // WO_CUT],
+                                      in_=wo_v[:, pr * 2 + i, lo:lo + C // WO_CUT])
 
         def load_k(g):
             nc.sync.dma_start(out=k_raw[:, 4 * g:4 * g + 4, :], in_=k_v[:, 4 * g:4 * g + 4, :])
@@ -498,20 +504,24 @@ def tile_selectivetransformerlayer_pb_kernel(tc, q_rot, k_rot, v, attention_mask
                         if hi == 8:
                             new_fin.append((cur[0][0], cur[1], cur[0][1]))
                             cur.clear()
-                    if not groups and not cur and not fin_list and not new_fin:
-                        if 0 not in lastb and s >= LASTB_AT:
-                            ps_l0 = psum.tile([P, 512], F32, tag=OP_TAG, bufs=OP_BUFS)
-                            lastb[0] = [ps_l0, 0]
-                        if 1 not in lastb and s >= LASTS_AT:
-                            ps_l1 = psum.tile([P, 512], F32, tag="s", bufs=S_BUFS)
-                            lastb[1] = [ps_l1, 0]
-                        if 2 not in lastb and s >= LASTS_AT:
-                            ps_l2 = psum.tile([P, 512], F32, tag="s", bufs=S_BUFS)
-                            lastb[2] = [ps_l2, 0]
+                    if s >= LASTS_AT:
+                        for ec in (1, 2):
+                            if ec not in lastb:
+                                ps_l = psum.tile([P, 512], F32, tag="s", bufs=S_BUFS)
+                                lastb[ec] = [ps_l, 0]
+                    if 0 not in lastb and s >= LASTB_AT and not groups and not cur and not fin_list and not new_fin:
+                        ps_l0 = psum.tile([P, 512], F32, tag=OP_TAG, bufs=OP_BUFS)
+                        lastb[0] = [ps_l0, 0]
                     for ec in lastb:
-                        while lastb[ec][1] < 8 and aq_slot.get(24 + lastb[ec][1], 999) < s:
+                        budget = 8
+                        if s < O_AT + NPAIR - 1:
+                            budget = LBN if ec > 0 else 0
+                        elif s <= O_AQ + NPAIR - 1 and ec == 0:
+                            budget = LB0
+                        while budget > 0 and lastb[ec][1] < 8 and aq_slot.get(24 + lastb[ec][1], 999) < s:
                             g = lastb[ec][1]
                             op_passes(NQB - 1, lastb[ec][0], ec, g, g + 1)
+                            budget -= 1
                             lastb[ec][1] = g + 1
                             if g == 7:
                                 op_finish(NQB - 1, lastb[ec][0], ec)

from contextlib import ExitStack
import math

import concourse.mybir as mybir
from concourse.masks import make_identity

F32 = mybir.dt.float32
BF16 = mybir.dt.bfloat16
U32 = mybir.dt.uint32
U8 = mybir.dt.uint8
FP8X4 = mybir.dt.float8_e4m3fn_x4
ALU = mybir.AluOpType
ACTF = mybir.ActivationFunctionType
AXIS = mybir.AxisListType

P = 128
H = 32
HKV = 4
S = 512
D = 128
E = 1536
C = H * D
NQB = S // P
UNITS_PER_QB = 8
NUNITS = NQB * UNITS_PER_QB
FLOPS = 2 * H * S * S * D * 2 + 2 * S * C * E

W_PLAN = (2, 1, 2, 1)
NPAIR = 64
W_START = 3
PE_MASK_TO = 42
NMASK2 = (0, 1, 1, 1)
OP_PV = True
VP_SLOT = 2
MT0 = -2
MT_SLOTS = (2, 10, 22, 38)
LASTB_AT = 60
LBN = 1
LB0 = 1
LASTS_AT = 64
WO_FIRST = 2
W_FREE = False
PE_MASK_FROM = 1
S_BUFS = 4
MISC_BUFS = 3
PV_TAG = "misc"
PV_BUFS = 3
OP_TAG = "op"
OP_BUFS = 1
ET_BUFS = 3
ET_TAG = "misc"
NMASK = (1, 1)
EXP_LAG = (1, 1)
O_ET = 2
NORM_V = (1, 1, 1, 1)
FC_V = (0, 0, 0, 0)
L_FC = 0
L_QU = 1
L_PV = 1
L_NM = 1
L_AT = 1
L_AC = 0
L_AQ = 2
L_WC = 0
L_WQ = 1
L_QC = 0
Q_AHEAD = 3
QN = 4
DUM_FROM = 99
DUM_TO = 99
DUM_N = 512
WARM = 5
WO_CUT = 2
PE_ORDER = ("et", "w", "at", "kqt", "mask0", "score0", "op", "pv", "mask1", "score1")
OPC = 2
OPC_LATE = 40
OPC2 = 4
OPC_LATE3 = 58
OPC3 = 4
SPLIT_S = False
SB_BUFS = 2
V_ORDER = ("vq", "front0", "fin", "front1", "norm", "max0", "max1", "fcopy", "aquant", "wcopy", "quant", "wquant")
S_ORDER = ("exp0", "exp1", "fcopy", "wcopy", "kcopy", "acopy", "norm", "qcopy")
W_ON_V = (0, 1, 0, 1)


def pe_masked(p, i):
    if p < PE_MASK_FROM:
        return False
    pat = NMASK if p < PE_MASK_TO else NMASK2
    return pat[(2 * p + i) % len(pat)] == 1


def FCOPY_V(p):
    return FC_V[p % 4] == 1


def norm_on_vector(u):
    return NORM_V[u % 4] == 1


def w_on_vector(w):
    return W_ON_V[w % 4] == 1


def tile_selectivetransformerlayer_pb_kernel(tc, q_rot, k_rot, v, attention_mask, wo, x, out):
    nc = tc.nc
    scale = 1.0 / math.sqrt(D)
    q_v = q_rot.rearrange("b h (n p) d -> p n (b h) d", p=P)
    k_v = k_rot.rearrange("b g (n p) d -> p (b g n) d", p=P)
    v_v = v.rearrange("b g (u p e) d -> p (b g u) e d", p=P, e=2)
    m_v = attention_mask.rearrange("a b (n p) k -> p (a b n) k", p=P)
    wo_v = wo.rearrange("(n p) c -> p n c", p=P)
    x_v = x.rearrange("b (n p) e -> p (b n) e", p=P)
    out_v = out.rearrange("b (n p) e -> p (b n) e", p=P)

    with ExitStack() as ctx:
        keep = ctx.enter_context(tc.tile_pool(name="keep", bufs=1))
        work = ctx.enter_context(tc.tile_pool(name="work", bufs=3))
        small = ctx.enter_context(tc.tile_pool(name="small", bufs=12))
        psum = ctx.enter_context(tc.psum_pool(name="psum", bufs=1))
        ctx.enter_context(tc.manual_schedule())

        k_raw = keep.tile([P, HKV * 4, D], BF16)
        mask_sb = keep.tile([P, NQB, S], BF16)
        v_raw = keep.tile([P, HKV * 2, 2, D], BF16)
        q_raws = {}

        def load_q_part(qb, c4):
            nc.sync.dma_start(out=q_raws[qb][:, c4 * 8:(c4 + 1) * 8, :], in_=q_v[:, qb, c4 * 8:(c4 + 1) * 8, :])

        def load_q(qb):
            q_raw = work.tile([P, H, D], BF16, tag="q_raw", bufs=2)
            q_raws[qb] = q_raw
            if qb > 0:
                for c4 in range(4):
                    load_q_part(qb, c4)

        ident_bf = keep.tile([P, P], BF16)
        make_identity(nc, ident_bf[:])
        ident_f = keep.tile([P, P], F32)
        make_identity(nc, ident_f[:])

        kT = keep.tile([P, HKV * S], BF16)
        if WARM > 0:
            zeros = keep.tile([P, S], BF16)
            nc.vector.memset(zeros[:], 0.0)
            ps_z = psum.tile([P, 512], F32, tag=OP_TAG, bufs=OP_BUFS)
            for rep in range(WARM):
                nc.tensor.matmul(out=ps_z[:], lhsT=zeros[:, 0:P], rhs=zeros[:], start=True, stop=True)
        mT = keep.tile([P, NQB, 4, P], F32)
        KS = {}
        MS = {}

        def pe_kt_list(g):
            ps_k = psum.tile([P, 4, P], BF16, tag="misc", bufs=MISC_BUFS)
            KS[g] = ps_k
            return [(ps_k[:, i, :], k_raw[:, g * 4 + i, :], ident_bf[:]) for i in range(4)]

        def s_kcopy(g):
            nc.scalar.copy(out=kT[:, g * S:(g + 1) * S], in_=KS[g][:].rearrange("p i k -> p (i k)"))

        def pe_mt_list(qb):
            ps_m = psum.tile([P, 4, P], BF16, tag="misc", bufs=MISC_BUFS)
            MS[qb] = ps_m
            return [(ps_m[:, t, :], mask_sb[:, qb, t * P:(t + 1) * P], ident_bf[:]) for t in range(4)]

        def s_mcopy(qb):
            nc.scalar.activation(out=mT[:, qb, :, :], in_=MS[qb][:], func=ACTF.Copy, scale=math.sqrt(D))

        v_grp = keep.tile([P, HKV, D, 4], BF16, align_bytes=64)
        vcodes = keep.tile([P, HKV * D], U32, align_bytes=64)
        vscales = keep.tile([P, HKV * D], U8, align_bytes=64)

        def v_prep_copy(g):
            nc.vector.tensor_copy(out=v_grp[:, g, :, :], in_=v_raw[:, 2 * g:2 * g + 2, :, :].rearrange("p u e d -> p d (u e)"))

        def v_prep_quant(g):
            nc.vector.quantize_mx(out=vcodes[:, g * D:(g + 1) * D].bitcast(FP8X4), scales=vscales[:, g * D:(g + 1) * D],
                                  in_=v_grp[:, g, :, :].rearrange("p d t -> p (d t)"))

        wcodes = keep.tile([P, 8, E], U32, align_bytes=64)
        wscales = keep.tile([P, 8, E], U8, align_bytes=64)
        x_sb = keep.tile([P, NQB, E], BF16)
        wo_raws = {}

        def load_wo(pr):
            for i in range(2):
                wo_raw = work.tile([P, C], BF16, tag="wo_raw", bufs=4)
                wo_raws[pr * 2 + i] = wo_raw
            for lo in range(0, C, C // WO_CUT):
                for i in range(2):
                    nc.sync.dma_start(out=wo_raws[pr * 2 + i][:, lo:lo + C // WO_CUT],
                                      in_=wo_v[:, pr * 2 + i, lo:lo + C // WO_CUT])

        def load_k(g):
            nc.sync.dma_start(out=k_raw[:, 4 * g:4 * g + 4, :], in_=k_v[:, 4 * g:4 * g + 4, :])

        def load_v(g):
            nc.sync.dma_start(out=v_raw[:, 2 * g:2 * g + 2, :, :], in_=v_v[:, 2 * g:2 * g + 2, :, :])

        load_q(0)
        load_k(0)
        nc.sync.dma_start(out=q_raws[0][:, 0:4, :], in_=q_v[:, 0, 0:4, :])
        nc.sync.dma_start(out=mask_sb[:, 0:1, :], in_=m_v[:, 0:1, :])
        nc.sync.dma_start(out=q_raws[0][:, 4:8, :], in_=q_v[:, 0, 4:8, :])
        load_k(1)
        load_v(0)
        load_q_part(0, 1)
        if WO_FIRST == 2:
            load_wo(0)
        load_k(2)
        load_v(1)
        load_q_part(0, 2)
        load_k(3)
        load_v(2)
        load_q_part(0, 3)
        load_v(3)
        nc.sync.dma_start(out=mask_sb[:, 1:4, :], in_=m_v[:, 1:4, :])
        if WO_FIRST != 2:
            load_wo(0)
        load_wo(1)

        PS = {}
        US = {u: {} for u in range(NUNITS)}
        QT = {}
        AS = {}
        RS = {}
        QS = {0: {}, 1: {}, 2: {}, 3: {}}
        WS = {}

        def tr(triple):
            nc.tensor.transpose(triple[0], triple[1], triple[2])

        def pe_qt_list(v):
            qb, a = divmod(v * QN, 32)
            ps_q = psum.tile([P, QN, P], BF16, tag="misc", bufs=MISC_BUFS)
            QT[v] = {"ps_q": ps_q}
            return [(ps_q[:, j, :], q_raws[qb][:, a + j, :], ident_bf[:]) for j in range(QN)]

        def s_qcopy(v):
            qT = work.tile([P, QN, P], BF16, tag="qT")
            nc.scalar.copy(out=qT[:], in_=QT[v]["ps_q"][:])
            QT[v]["qT"] = qT

        def pe_mask(p, i):
            if SPLIT_S and pe_masked(p, i) or not SPLIT_S:
                ps_s = psum.tile([P, S], F32, tag="s", bufs=S_BUFS)
            else:
                ps_s = psum.tile([P, S], F32, tag="sb", bufs=SB_BUFS)
            PS[p]["ps_s%d" % i] = ps_s
            if pe_masked(p, i):
                for t in range(4):
                    nc.tensor.matmul(out=ps_s[:, t * P:(t + 1) * P], lhsT=mT[:, p // 16, t, :], rhs=ident_f[:],
                                     start=(t == 0), stop=False, is_transpose=True)

        def pe_score(p, i):
            u = p // 2
            g = (u % UNITS_PER_QB) // 2
            nc.tensor.matmul(out=PS[p]["ps_s%d" % i][:], lhsT=QT[(2 * p + i) // QN]["qT"][:, (2 * p + i) % QN, :],
                             rhs=kT[:, g * S:(g + 1) * S], start=not pe_masked(p, i), stop=True)

        def v_front(p, i):
            if pe_masked(p, i):
                return
            t = work.tile([P, S], F32, tag="t")
            nc.vector.scalar_tensor_tensor(out=t[:], in0=PS[p]["ps_s%d" % i][:], scalar=scale,
                                           in1=mask_sb[:, p // 16, :], op0=ALU.mult, op1=ALU.add)
            PS[p]["t%d" % i] = t

        def v_max(p, i):
            negm = small.tile([P, 1], F32, tag="negm")
            PS[p]["negm%d" % i] = negm
            if pe_masked(p, i):
                rmax = small.tile([P, 1], F32, tag="rmax")
                nc.vector.tensor_reduce(out=rmax[:], in_=PS[p]["ps_s%d" % i][:], axis=AXIS.X, op=ALU.max)
                nc.gpsimd.tensor_scalar(out=negm[:], in0=rmax[:], scalar1=-scale, scalar2=0.0,
                                        op0=ALU.mult, op1=ALU.add)
            else:
                nc.vector.tensor_reduce(out=negm[:], in_=PS[p]["t%d" % i][:], axis=AXIS.X, op=ALU.max, negate=True)

        def s_exp(p, i):
            if "e" not in PS[p]:
                e = work.tile([P, 2, S], BF16, tag="e")
                PS[p]["e"] = e
                if p % 2 == 0:
                    rowsum = small.tile([P, 4], F32, tag="rowsum")
                    US[p // 2]["rowsum"] = rowsum
            src = PS[p]["ps_s%d" % i] if pe_masked(p, i) else PS[p]["t%d" % i]
            nc.scalar.activation(out=PS[p]["e"][:, i, :], in_=src[:], func=ACTF.Exp,
                                 bias=PS[p]["negm%d" % i][:], scale=scale if pe_masked(p, i) else 1.0,
                                 accum_out=US[p // 2]["rowsum"][:, 2 * (p % 2) + i:2 * (p % 2) + i + 1])

        def pe_et_list(p):
            ps_t = psum.tile([P, 2, 2, P], F32, tag=ET_TAG, bufs=ET_BUFS)
            PS[p]["ps_t"] = ps_t
            e32 = PS[p]["e"][:].rearrange("p i s -> p (i s)").bitcast(F32)
            return [(ps_t[:, i, u, :], e32[:, (2 * i + u) * P:(2 * i + u + 1) * P], ident_f[:])
                    for i in range(2) for u in range(2)]

        def s_fcopy(p):
            grp = work.tile([P, 8 * P], BF16, tag="grp", align_bytes=64)
            (nc.vector.tensor_copy if FCOPY_V(p) else nc.scalar.copy)(out=grp[:].bitcast(F32).rearrange("p (i q u) -> p i q u", i=2, u=2),
                           in_=PS[p]["ps_t"][:].rearrange("p i u q -> p i q u"))
            PS[p]["grp"] = grp

        def v_quant(p):
            ecodes = work.tile([P, 2 * P], U32, tag="ecodes", bufs=4, align_bytes=64)
            escales = work.tile([P, 2 * P], U8, tag="escales", bufs=4, align_bytes=64)
            nc.vector.quantize_mx(out=ecodes[:].bitcast(FP8X4), scales=escales[:],
                                  in_=PS[p]["grp"][:])
            PS[p]["ecodes"] = ecodes
            PS[p]["escales"] = escales
            if p % 2 == 1:
                r = small.tile([P, 4], F32, tag="r")
                nc.vector.reciprocal(out=r[:], in_=US[p // 2]["rowsum"][:])
                US[p // 2]["r"] = r

        def pe_pv(u):
            g = (u % UNITS_PER_QB) // 2
            ps_o = psum.tile([P, 4, P], F32, tag=PV_TAG, bufs=PV_BUFS)
            for j in range(4):
                p, i = 2 * u + j // 2, j % 2
                nc.tensor.matmul_mx(out=ps_o[:, j, :],
                                    lhsT=PS[p]["ecodes"][:, i * P:(i + 1) * P].bitcast(FP8X4),
                                    lhsT_scale=PS[p]["escales"][:, i * P:(i + 1) * P],
                                    rhs=vcodes[:, g * D:(g + 1) * D].bitcast(FP8X4),
                                    rhs_scale=vscales[:, g * D:(g + 1) * D],
                                    start=True, stop=True)
            US[u]["ps_o"] = ps_o

        def norm(u):
            rr = u // 2
            gi = u % 2
            if gi == 0:
                attn2 = work.tile([P, 2, 4, P], BF16, tag="attn2", bufs=2)
                RS[rr] = {"attn2": attn2}
            attn2 = RS[rr]["attn2"]
            ps_o = US[u]["ps_o"]
            r = US[u]["r"]
            nv = 4 if norm_on_vector(u) else 0
            if u == NUNITS - 1:
                nv = 2
            if nv > 0:
                nc.vector.tensor_tensor(out=attn2[:, gi, 0:nv, :], in0=ps_o[:, 0:nv, :],
                                        in1=r[:, 0:nv].unsqueeze(2).to_broadcast([P, nv, P]), op=ALU.mult)
            if nv < 4:
                for j in range(nv, 4):
                    nc.scalar.activation(out=attn2[:, gi, j, :], in_=ps_o[:, j, :],
                                         func=ACTF.Copy, scale=r[:, j:j + 1])

        def piece(d):
            if d < 0:
                return None
            if d >= NPAIR - 4:
                return {NPAIR - 3: (15, 0, 1), NPAIR - 1: (15, 1, 2)}.get(d)
            return (d // 4, 0, 2) if d % 4 == 3 else None

        def pe_at_list(pc):
            rr, lo, hi = pc
            ps_a = psum.tile([P, 2, 2, P], F32, tag="misc", bufs=MISC_BUFS)
            AS[pc] = {"ps_a": ps_a}
            a32 = RS[rr]["attn2"][:].rearrange("p i j d -> p (i j d)").bitcast(F32)
            return [(ps_a[:, i, u, :], a32[:, (2 * i + u) * P:(2 * i + u + 1) * P], ident_f[:])
                    for i in range(lo, hi) for u in range(2)]

        def s_acopy(pc):
            rr, lo, hi = pc
            ag = work.tile([P, 2, 4 * P], BF16, tag="ag", bufs=2, align_bytes=64)
            for_words = ag[:].bitcast(F32).rearrange("p i (q u) -> p i q u", u=2)
            nc.scalar.copy(out=for_words[:, lo:hi, :, :],
                           in_=AS[pc]["ps_a"][:, lo:hi, :, :].rearrange("p i u q -> p i q u"))
            AS[pc]["ag"] = ag

        def v_aquant(pc):
            rr, lo, hi = pc
            qb, k4 = divmod(rr, 4)
            if k4 == 0:
                acodes = work.tile([P, 8 * P], U32, tag="acodes", bufs=4, align_bytes=64)
                ascales = work.tile([P, 8 * P], U8, tag="ascales", bufs=4, align_bytes=64)
                QS[qb]["acodes"] = acodes
                QS[qb]["ascales"] = ascales
            a, b = (k4 * 2 + lo) * P, (k4 * 2 + hi) * P
            nc.vector.quantize_mx(out=QS[qb]["acodes"][:, a:b].bitcast(FP8X4),
                                  scales=QS[qb]["ascales"][:, a:b],
                                  in_=AS[pc]["ag"][:, lo:hi, :].rearrange("p i c -> p (i c)"))

        def pe_w(w):
            pr, g = divmod(w, 8)
            ps_w = psum.tile([P, 2, 2 * P], F32, tag="misc", bufs=MISC_BUFS)
            for i in range(2):
                w32 = wo_raws[pr * 2 + i][:].bitcast(F32)
                for uu in range(2):
                    lo = g * 256 + uu * P
                    nc.tensor.transpose(ps_w[:, uu, i * P:(i + 1) * P], w32[:, lo:lo + P], ident_f[:])
            WS[w] = {"ps_w": ps_w}
            if g == 7 and pr + 2 < 6:
                load_wo(pr + 2)

        def w_copy(w):
            wg = work.tile([P, 1024], BF16, tag="wg", align_bytes=64)
            dst = wg[:].bitcast(F32).rearrange("p (e u) -> p e u", u=2)
            src = WS[w]["ps_w"][:].rearrange("p u e -> p e u")
            if w_on_vector(w):
                nc.vector.tensor_copy(out=dst, in_=src)
            else:
                nc.scalar.copy(out=dst, in_=src)
            WS[w]["wg"] = wg

        def v_wquant(w):
            pr, g = divmod(w, 8)
            nc.vector.quantize_mx(out=wcodes[:, g, pr * 256:(pr + 1) * 256].bitcast(FP8X4),
                                  scales=wscales[:, g, pr * 256:(pr + 1) * 256], in_=WS[w]["wg"][:])

        def op_passes(qb, ps, ec, g_lo, g_hi):
            for g in range(g_lo, g_hi):
                nc.tensor.matmul_mx(out=ps[:],
                                    lhsT=QS[qb]["acodes"][:, g * P:(g + 1) * P].bitcast(FP8X4),
                                    lhsT_scale=QS[qb]["ascales"][:, g * P:(g + 1) * P],
                                    rhs=wcodes[:, g, ec * 512:(ec + 1) * 512].bitcast(FP8X4),
                                    rhs_scale=wscales[:, g, ec * 512:(ec + 1) * 512],
                                    start=(g == 0), stop=(g == 7))

        def op_finish(qb, ps, ec):
            o_sb = work.tile([P, 512], F32, tag="o_sb")
            nc.vector.tensor_tensor(out=o_sb[:], in0=ps[:], in1=x_sb[:, qb, ec * 512:(ec + 1) * 512], op=ALU.add)
            nc.sync.dma_start(out=out_v[:, qb, ec * 512:(ec + 1) * 512], in_=o_sb[:])

        O_FC = O_ET + L_FC
        O_QU = O_FC + L_QU
        O_PV = O_QU + L_PV
        O_NM = O_PV + L_NM
        O_AT = O_NM + L_AT
        O_AC = O_AT + L_AC
        O_AQ = O_AC + L_AQ
        w_next = 0
        w_slot = {}
        aq_slot = {}
        groups = [(qb, ec) for qb in range(NQB - 1) for ec in range(3)]
        lastb = {}
        n_last = 0
        cur = []
        fin_list = []
        new_fin = []
        MT_SLOT = {MT0: 0, MT_SLOTS[1]: 1, MT_SLOTS[2]: 2, MT_SLOTS[3]: 3}
        K_SLOT = {-Q_AHEAD: 0, 0: 1, 4: 2, 8: 3}
        last = NPAIR + O_AQ + 1
        s = -Q_AHEAD
        while s < last or groups or fin_list or new_fin or n_last < 3:
            have_next = 0 <= s + 1 < NPAIR
            if have_next:
                PS[s + 1] = {}
            at_now = piece(s - O_AT) is not None
            qt_now = (s + Q_AHEAD) % (QN // 2) == 0 and 0 <= (s + Q_AHEAD) // (QN // 2) < 128 // QN
            n_misc = (s in K_SLOT) + (s in MT_SLOT) + at_now + qt_now
            w_now = []
            if s >= W_START:
                for rep in range(W_PLAN[s % 4] if W_FREE else min(W_PLAN[s % 4], 2 - n_misc)):
                    if w_next < 48:
                        w_now.append(w_next)
                        w_slot[w_next] = s
                        w_next += 1
            for step in PE_ORDER:
                if step == "et" and 0 <= s - O_ET < NPAIR:
                    for triple in pe_et_list(s - O_ET):
                        tr(triple)
                elif step == "kqt":
                    if s in K_SLOT:
                        for triple in pe_kt_list(K_SLOT[s]):
                            tr(triple)
                    if s in MT_SLOT:
                        for triple in pe_mt_list(MT_SLOT[s]):
                            tr(triple)
                    if qt_now:
                        for triple in pe_qt_list((s + Q_AHEAD) // (QN // 2)):
                            tr(triple)
                elif step == "dum" and DUM_FROM <= s < DUM_TO:
                    ps_d = psum.tile([P, 512], F32, tag=OP_TAG, bufs=OP_BUFS)
                    nc.tensor.matmul(out=ps_d[:, 0:DUM_N], lhsT=ident_bf[:], rhs=kT[:, 0:DUM_N], start=True, stop=True)
                elif step == "w":
                    for w in w_now:
                        pe_w(w)
                elif step == "at" and at_now:
                    for triple in pe_at_list(piece(s - O_AT)):
                        tr(triple)
                elif step in ("mask0", "mask1") and have_next:
                    pe_mask(s + 1, int(step[4]))
                elif step in ("score0", "score1") and have_next:
                    pe_score(s + 1, int(step[5]))
                elif step == "pv" and (s - O_PV) % 2 == 1 and 0 <= s - O_PV < NPAIR:
                    pe_pv((s - O_PV) // 2)
                elif step == "op" and (not OP_PV or (s - O_PV) % 2 == 1 or s >= NPAIR):
                    ready = [gr for gr in groups
                             if w_slot.get(16 * gr[1] + 15, 999) + L_WC + L_WQ < s and aq_slot.get(8 * gr[0] + 7, 999) < s]
                    if ready and not cur and not fin_list:
                        cur.append(ready[0])
                        groups = [gr for gr in groups if gr != cur[0]]
                        ps_p = psum.tile([P, 512], F32, tag=OP_TAG, bufs=OP_BUFS)
                        cur.extend([ps_p, 0])
                    if cur:
                        hi = min(8, cur[2] + (OPC if s < OPC_LATE else OPC2 if s < OPC_LATE3 else OPC3))
                        op_passes(cur[0][0], cur[1], cur[0][1], cur[2], hi)
                        cur[2] = hi
                        if hi == 8:
                            new_fin.append((cur[0][0], cur[1], cur[0][1]))
                            cur.clear()
                    if s >= LASTS_AT:
                        for ec in (1, 2):
                            if ec not in lastb:
                                ps_l = psum.tile([P, 512], F32, tag="s", bufs=S_BUFS)
                                lastb[ec] = [ps_l, 0]
                    if 0 not in lastb and s >= LASTB_AT and not groups and not cur and not fin_list and not new_fin:
                        ps_l0 = psum.tile([P, 512], F32, tag=OP_TAG, bufs=OP_BUFS)
                        lastb[0] = [ps_l0, 0]
                    for ec in lastb:
                        budget = 8
                        if s < O_AT + NPAIR - 1:
                            budget = LBN if ec > 0 else 0
                        elif s <= O_AQ + NPAIR - 1 and ec == 0:
                            budget = LB0
                        while budget > 0 and lastb[ec][1] < 8 and aq_slot.get(24 + lastb[ec][1], 999) < s:
                            g = lastb[ec][1]
                            op_passes(NQB - 1, lastb[ec][0], ec, g, g + 1)
                            budget -= 1
                            lastb[ec][1] = g + 1
                            if g == 7:
                                op_finish(NQB - 1, lastb[ec][0], ec)
                                n_last += 1
            for step in V_ORDER:
                if step in ("front0", "front1") and 0 <= s < NPAIR:
                    v_front(s, int(step[5]))
                elif step in ("max0", "max1") and 0 <= s < NPAIR:
                    v_max(s, int(step[3]))
                elif step == "vq":
                    if (s - VP_SLOT) % 4 == 0 and 0 <= (s - VP_SLOT) // 4 < HKV:
                        v_prep_copy((s - VP_SLOT) // 4)
                    if (s - VP_SLOT) % 4 == 1 and 0 <= (s - VP_SLOT) // 4 < HKV:
                        v_prep_quant((s - VP_SLOT) // 4)
                elif step == "quant" and 0 <= s - O_QU < NPAIR:
                    v_quant(s - O_QU)
                elif step == "wcopy":
                    for w in range(48):
                        if w_slot.get(w) == s - L_WC and w_on_vector(w):
                            w_copy(w)
                elif step == "fcopy" and 0 <= s - O_FC < NPAIR and FCOPY_V(s - O_FC):
                    s_fcopy(s - O_FC)
                elif step == "wquant":
                    for w in range(48):
                        if w_slot.get(w) == s - L_WC - L_WQ:
                            v_wquant(w)
                elif step == "norm" and (s - O_NM) % 2 == 1 and 0 <= s - O_NM < NPAIR and norm_on_vector((s - O_NM) // 2):
                    norm((s - O_NM) // 2)
                elif step == "aquant" and piece(s - O_AQ) is not None:
                    pc = piece(s - O_AQ)
                    v_aquant(pc)
                    for i in range(pc[1], pc[2]):
                        aq_slot[2 * pc[0] + i] = s
                elif step == "fin":
                    todo = fin_list[:]
                    fin_list = new_fin
                    new_fin = []
                    for item in todo:
                        op_finish(item[0], item[1], item[2])
            for step in S_ORDER:
                if step in ("exp0", "exp1"):
                    i = int(step[3])
                    if 0 <= s - EXP_LAG[i] < NPAIR:
                        s_exp(s - EXP_LAG[i], i)
                elif step == "fcopy" and 0 <= s - O_FC < NPAIR and not FCOPY_V(s - O_FC):
                    s_fcopy(s - O_FC)
                elif step == "kcopy":
                    if s - L_QC in K_SLOT:
                        s_kcopy(K_SLOT[s - L_QC])
                    if s - L_QC in MT_SLOT:
                        s_mcopy(MT_SLOT[s - L_QC])
                elif step == "wcopy":
                    for w in range(48):
                        if w_slot.get(w) == s - L_WC and not w_on_vector(w):
                            w_copy(w)
                elif step == "acopy" and piece(s - O_AC) is not None:
                    s_acopy(piece(s - O_AC))
                elif step == "qcopy" and (s - L_QC + Q_AHEAD) % (QN // 2) == 0 and 0 <= (s - L_QC + Q_AHEAD) // (QN // 2) < 128 // QN:
                    s_qcopy((s - L_QC + Q_AHEAD) // (QN // 2))
                elif step == "norm" and (s - O_NM) % 2 == 1 and 0 <= s - O_NM < NPAIR and not norm_on_vector((s - O_NM) // 2):
                    norm((s - O_NM) // 2)
            if s == 0:
                load_q(1)
            if s == 6:
                nc.sync.dma_start(out=x_sb[:], in_=x_v)
            if s == 13:
                load_q(2)
            if s == 29:
                load_q(3)
            s += 1
